import numpy as np
import ml_dtypes


def mxq(x, axis, fmt="e4m3"):
    dtype, down = {"e4m3": (ml_dtypes.float8_e4m3fn, 7), "e5m2": (ml_dtypes.float8_e5m2, 14)}[fmt]
    v = np.moveaxis(np.asarray(x, np.float32).astype(ml_dtypes.bfloat16).astype(np.float64), axis, -1)
    blocks = v.reshape(v.shape[:-1] + (-1, 32))
    amax = np.abs(blocks).max(-1, keepdims=True)
    byte = np.maximum(np.where(amax > 0, np.frexp(amax)[1] - 1 + 127, 0) - down, 1)
    scale = np.exp2(byte - 127.0)
    codes = (blocks / scale).astype(np.float32).astype(dtype).astype(np.float64)
    return np.moveaxis((codes * scale).reshape(v.shape), -1, axis)


WIDE = False


def mx_kscale(k):
    if not WIDE:
        return np.ones(k)
    levels = np.array([10, -10, 5, -5, 0])
    a = np.random.permutation(np.resize(levels, k // 512 * 4)).reshape(k // 512, 4)
    idx = np.arange(k)
    return np.exp2(a[idx // 512, idx % 128 // 32])


BF16 = ml_dtypes.bfloat16


def bf(x):
    return np.asarray(x, np.float32).astype(BF16)


def f64(x):
    return np.asarray(x).astype(np.float64)


B, S, L, H = 2, 256, 8, 512
F = 2 * H
VERT = np.array([[-1, -1, -1], [-1, -1, 1], [-1, 1, -1], [-1, 1, 1], [1, -1, -1], [1, -1, 1], [1, 1, -1], [1, 1, 1]], np.float64) * (np.pi / 2)


def sigmoid(v):
    return 1.0 / (1.0 + np.exp(-v))


def routing_matrix(p, t):
    mid = (p[:, None, :] + p[None, :, :]) * 0.5
    cx, cy, cz = mid[..., 0], mid[..., 1], mid[..., 2]
    f = (np.sin(cx) * np.cos(cy) + np.sin(cy) * np.cos(cz) + np.sin(cz) * np.cos(cx)) - t
    r = sigmoid(2.0 * f)
    r = np.where(np.eye(L) > 0, 1.0, r)
    return r / (r.sum(axis=1, keepdims=True) + 1e-6)


def setup_inputs():
    s = mx_kscale(H)
    return {"x": bf(np.random.standard_normal((B, S, L, H)) * s),
            "limb_positions": bf(VERT + 0.2 * np.random.standard_normal(VERT.shape)),
            "channel_threshold": bf(np.atleast_1d(0.3 + 0.1 * np.random.standard_normal())),
            "W_route": bf(np.random.standard_normal((H, H)) * 2.0 / np.sqrt(H) * s[:, None] / s[None, :]),
            "b_route": bf(np.random.standard_normal(H) * 0.5 * s),
            "W_gate": bf(np.random.standard_normal((H, F)) / np.sqrt(H) / np.concatenate([s, s])[None, :]),
            "b_gate": bf(np.random.standard_normal(H) * 0.5)}


def reference(x, limb_positions, channel_threshold, W_route, b_route, W_gate, b_gate):
    x = f64(x)
    routing = routing_matrix(f64(limb_positions), f64(channel_threshold))
    xq = mxq(x, 3, "e4m3")
    projected = (xq @ mxq(f64(W_route), 1, "e4m3").T) + f64(b_route)
    routed = sum(routing[:, j][None, None, :, None] * projected[:, :, j:j + 1, :] for j in range(L))
    gate_in = np.concatenate([xq, mxq(routed, 3, "e4m3")], axis=-1)
    gate = sigmoid((gate_in @ mxq(f64(W_gate), 1, "e4m3").T) + f64(b_gate))
    return gate * routed + (1.0 - gate) * x

@@ -1,0 +1,350 @@
+import math
+from contextlib import ExitStack
+
+import concourse.masks as masks
+import concourse.mybir as mybir
+
+F32 = mybir.dt.float32
+BF16 = mybir.dt.bfloat16
+I32 = mybir.dt.int32
+U32 = mybir.dt.uint32
+U8 = mybir.dt.uint8
+FP8X4 = mybir.dt.float8_e4m3fn_x4
+ALU = mybir.AluOpType
+ACT = mybir.ActivationFunctionType
+AXIS_X = mybir.AxisListType.X
+
+P = 128
+PACK = 4
+LIMBS = 8
+FEATURES = 512
+CHUNKS = FEATURES // P
+ROWS = 2 * 256 * LIMBS
+TILES = ROWS // P
+POSITIONS = P // LIMBS
+GROUP_TILES = 4
+GROUP = GROUP_TILES * P
+GROUPS = TILES // GROUP_TILES
+PAIRS = LIMBS * LIMBS
+PSUM_BANKS = 8
+
+FLOPS = 2 * ROWS * FEATURES * FEATURES + 2 * ROWS * 2 * FEATURES * FEATURES + 2 * ROWS * LIMBS * FEATURES
+
+
+def tile_tpmslimbrouter_pa_t_kernel(
+    tc, x, limb_positions, channel_threshold, W_route, b_route, W_gate, b_gate, out
+):
+    nc = tc.nc
+    x_dram = x.rearrange("b s l h -> (b s l) h").rearrange("(n p) h -> p n h", p=P)
+    out_dram = out.rearrange("b s l h -> (b s l) h").rearrange("(n p) h -> p n h", p=P)
+
+    with ExitStack() as ctx:
+        keep = ctx.enter_context(tc.tile_pool(name="keep", bufs=1))
+        ring = ctx.enter_context(tc.tile_pool(name="ring", bufs=2))
+        banks = ctx.enter_context(tc.psum_pool(name="banks", bufs=PSUM_BANKS))
+        ctx.enter_context(tc.manual_schedule())
+
+        route_rows = keep.tile([P, CHUNKS, FEATURES], BF16)
+        gate_rows = keep.tile([P, CHUNKS, 2 * FEATURES], BF16)
+        x_rows = keep.tile([P, TILES, FEATURES], BF16)
+
+        def load_x(g):
+            tiles = slice(g * GROUP_TILES, (g + 1) * GROUP_TILES)
+            nc.sync.dma_start(out=x_rows[:, tiles, :], in_=x_dram[:, tiles, :])
+
+        nc.sync.dma_start(
+            out=route_rows[:].rearrange("p (u e) k -> p u (e k)", u=2),
+            in_=W_route.rearrange("(u p e) k -> p u (e k)", u=2, p=P),
+        )
+        load_x(0)
+        load_x(1)
+        nc.sync.dma_start(
+            out=gate_rows[:].rearrange("p (u e) k -> p u (e k)", u=2),
+            in_=W_gate.rearrange("(u p e) k -> p u (e k)", u=2, p=P),
+        )
+        for g in range(2, GROUPS):
+            load_x(g)
+
+        positions_bf = keep.tile([P, LIMBS, 3], BF16)
+        threshold_bf = keep.tile([P, 1], BF16)
+        b_route_bf = keep.tile([P, FEATURES], BF16)
+        b_gate_bf = keep.tile([P, CHUNKS], BF16)
+        nc.scalar.dma_start(
+            out=positions_bf[:].rearrange("p l c -> p (l c)"),
+            in_=limb_positions.rearrange("l c -> (l c)").partition_broadcast(P),
+        )
+        nc.scalar.dma_start(out=threshold_bf[:], in_=channel_threshold.partition_broadcast(P))
+        nc.scalar.dma_start(out=b_route_bf[:], in_=b_route.partition_broadcast(P))
+        nc.scalar.dma_start(
+            out=b_gate_bf[:].rearrange("p (u e) -> p u e", u=2),
+            in_=b_gate.rearrange("(u p e) -> p u e", u=2, p=P),
+        )
+
+        identity = keep.tile([P, P], F32)
+        masks.make_identity(nc, identity[:])
+        bias_route = keep.tile([P, FEATURES], F32)
+        nc.gpsimd.tensor_copy(
+            out=bias_route[:].rearrange("q (u e p) -> q u e p", u=2, e=2),
+            in_=b_route_bf[:].rearrange("q (u p e) -> q u e p", u=2, e=2),
+        )
+        bias_gate = keep.tile([P, CHUNKS], F32)
+        nc.gpsimd.tensor_copy(out=bias_gate[:], in_=b_gate_bf[:])
+
+        def transpose_rows(rows_words, grouped):
+            grouped_words = grouped.bitcast(F32)
+            for half in range(2):
+                bank = banks.tile([P, 2, 2, P], F32, tag="bank")
+                for i in range(2):
+                    for u in range(2):
+                        nc.tensor.transpose(
+                            bank[:, i, u, :], rows_words[:, 2 * half + i, u * P : (u + 1) * P], identity[:]
+                        )
+                nc.scalar.copy(
+                    out=grouped_words[:, half * 2 * P : (half + 1) * 2 * P, :].rearrange(
+                        "p (i r) u -> p i r u", i=2
+                    ),
+                    in_=bank[:].rearrange("p i u r -> p i r u"),
+                )
+
+        def quantise(grouped, codes, scales):
+            nc.vector.quantize_mx(
+                out=codes.bitcast(FP8X4), scales=scales, in_=grouped.rearrange("p r t -> p (r t)")
+            )
+
+        coords = keep.tile([P, 4, LIMBS], F32)
+        nc.vector.tensor_copy(out=coords[:, 0:3, :], in_=positions_bf[:].rearrange("p l c -> p c l"))
+        nc.vector.tensor_copy(out=coords[:, 3, :], in_=positions_bf[:, :, 0])
+        pair_sum = keep.tile([P, 4, LIMBS, LIMBS], F32)
+        pair_shape = [P, 4, LIMBS, LIMBS]
+        nc.vector.tensor_tensor(
+            out=pair_sum[:],
+            in0=coords[:].unsqueeze(3).to_broadcast(pair_shape),
+            in1=coords[:].unsqueeze(2).to_broadcast(pair_shape),
+            op=ALU.add,
+        )
+        turns = keep.tile([P, 2, 3 * PAIRS], F32)
+        per_turn = 1.0 / (4.0 * math.pi)
+        nc.vector.tensor_scalar_mul(
+            out=turns[:, 0, :], in0=pair_sum[:, 0:3].rearrange("p c i j -> p (c i j)"), scalar1=per_turn
+        )
+        nc.vector.tensor_scalar(
+            out=turns[:, 1, :],
+            in0=pair_sum[:, 1:4].rearrange("p c i j -> p (c i j)"),
+            scalar1=per_turn,
+            scalar2=0.25,
+            op0=ALU.mult,
+            op1=ALU.add,
+        )
+        whole_int = keep.tile([P, 2, 3 * PAIRS], I32)
+        whole = keep.tile([P, 2, 3 * PAIRS], F32)
+        part = keep.tile([P, 2, 3 * PAIRS], F32)
+        flipped = keep.tile([P, 2, 3 * PAIRS], F32)
+        folded = keep.tile([P, 2, 3 * PAIRS], F32)
+        nc.vector.tensor_copy(out=whole_int[:], in_=turns[:])
+        nc.vector.tensor_copy(out=whole[:], in_=whole_int[:])
+        nc.vector.tensor_tensor(out=part[:], in0=turns[:], in1=whole[:], op=ALU.subtract)
+        nc.vector.scalar_tensor_tensor(
+            out=flipped[:], in0=part[:], scalar=0.5, in1=part[:], op0=ALU.is_gt, op1=ALU.subtract
+        )
+        nc.vector.scalar_tensor_tensor(
+            out=folded[:], in0=flipped[:], scalar=0.5, in1=flipped[:], op0=ALU.is_gt, op1=ALU.subtract
+        )
+        waves = keep.tile([P, 2, 3, PAIRS], F32)
+        nc.scalar.activation(
+            out=waves[:].rearrange("p w c n -> p w (c n)"), in_=folded[:], func=ACT.Sin, scale=2.0 * math.pi
+        )
+        products = keep.tile([P, 3, PAIRS], F32)
+        gyroid = keep.tile([P, PAIRS], F32)
+        nc.vector.tensor_tensor(out=products[:], in0=waves[:, 0], in1=waves[:, 1], op=ALU.mult)
+        nc.vector.tensor_reduce(
+            out=gyroid[:], in_=products[:].rearrange("p c n -> p n c"), axis=AXIS_X, op=ALU.add
+        )
+        minus_2_threshold = keep.tile([P, 1], F32)
+        nc.vector.tensor_scalar_mul(out=minus_2_threshold[:], in0=threshold_bf[:], scalar1=-2.0)
+        own_limb = keep.tile([P, LIMBS], F32)
+        same_position = keep.tile([P, POSITIONS], F32)
+        nc.vector.tensor_reduce(
+            out=own_limb[:], in_=identity[:].rearrange("q (b j) -> q j b", j=LIMBS), axis=AXIS_X, op=ALU.add
+        )
+        nc.vector.tensor_reduce(
+            out=same_position[:], in_=identity[:].rearrange("q (b j) -> q b j", j=LIMBS), axis=AXIS_X, op=ALU.add
+        )
+
+        x_words = x_rows[:].bitcast(F32)
+        x_grouped = {}
+        x_codes = {}
+        x_scales = {}
+
+        def transpose_x(g):
+            x_grouped[g] = ring.tile([P, GROUP, PACK], BF16, name="x_grouped", bufs=3, align_bytes=64)
+            transpose_rows(x_words[:, g * GROUP_TILES : (g + 1) * GROUP_TILES, :], x_grouped[g][:])
+
+        def quantise_x(g):
+            x_codes[g] = ring.tile([P, GROUP], U32, name="x_codes", bufs=3, align_bytes=64)
+            x_scales[g] = ring.tile([P, GROUP], U8, name="x_scales", bufs=3, align_bytes=64)
+            quantise(x_grouped[g][:], x_codes[g][:], x_scales[g][:])
+
+        route_grouped = keep.tile([P, FEATURES, PACK], BF16, align_bytes=64)
+        route_codes = keep.tile([P, FEATURES], U32, align_bytes=64)
+        route_scales = keep.tile([P, FEATURES], U8, align_bytes=64)
+        transpose_rows(route_rows[:].bitcast(F32), route_grouped[:])
+        transpose_x(0)
+        quantise(route_grouped[:], route_codes[:], route_scales[:])
+        quantise_x(0)
+
+        r = keep.tile([P, LIMBS, LIMBS], F32)
+        r_flat = r[:].rearrange("p i j -> p (i j)")
+        nc.scalar.activation(
+            out=r_flat, in_=gyroid[:], func=ACT.Sigmoid, bias=minus_2_threshold[:, 0:1], scale=2.0
+        )
+        nc.vector.memset(r_flat[:, 0 : PAIRS : LIMBS + 1], 1.0)
+        row_sum = keep.tile([P, LIMBS], F32)
+        inverse = keep.tile([P, LIMBS], F32)
+        nc.vector.tensor_reduce(out=row_sum[:], in_=r[:], axis=AXIS_X, op=ALU.add)
+        nc.vector.tensor_scalar_add(out=row_sum[:], in0=row_sum[:], scalar1=1e-6)
+        nc.vector.reciprocal(out=inverse[:], in_=row_sum[:])
+        picked = keep.tile([P, LIMBS, LIMBS], F32)
+        weights = keep.tile([P, LIMBS], F32)
+        nc.vector.tensor_tensor(
+            out=picked[:], in0=r[:], in1=own_limb[:].unsqueeze(1).to_broadcast([P, LIMBS, LIMBS]), op=ALU.mult
+        )
+        nc.vector.tensor_reduce(out=weights[:], in_=picked[:], axis=AXIS_X, op=ALU.add)
+        nc.vector.tensor_tensor(out=weights[:], in0=weights[:], in1=inverse[:], op=ALU.mult)
+        mixer = keep.tile([P, POSITIONS, LIMBS], F32)
+        nc.vector.tensor_tensor(
+            out=mixer[:],
+            in0=same_position[:].unsqueeze(2).to_broadcast([P, POSITIONS, LIMBS]),
+            in1=weights[:].unsqueeze(1).to_broadcast([P, POSITIONS, LIMBS]),
+            op=ALU.mult,
+        )
+        mixer_flat = mixer[:].rearrange("q b i -> q (b i)")
+
+        projected = {}
+        routed_codes = {}
+        routed_scales = {}
+        routed_grouped = {}
+        difference = {}
+        update = {}
+
+        def project(g):
+            projected[g] = ring.tile([P, GROUP_TILES, FEATURES], F32, name="projected")
+            for a in range(GROUP_TILES):
+                tokens = slice(a * P, (a + 1) * P)
+                bank = banks.tile([P, FEATURES], F32, tag="bank")
+                nc.tensor.matmul_mx(
+                    out=bank[:],
+                    lhsT=x_codes[g][:, tokens].bitcast(FP8X4),
+                    lhsT_scale=x_scales[g][:, tokens],
+                    rhs=route_codes[:].bitcast(FP8X4),
+                    rhs_scale=route_scales[:],
+                    start=True,
+                    stop=True,
+                )
+                nc.vector.tensor_tensor(out=projected[g][:, a, :], in0=bank[:], in1=bias_route[:], op=ALU.add)
+
+        def start_routed(g):
+            routed_grouped[g] = ring.tile([P, GROUP, PACK], BF16, name="routed_grouped", align_bytes=64)
+            routed_codes[g] = ring.tile([P, GROUP], U32, name="routed_codes", align_bytes=64)
+            routed_scales[g] = ring.tile([P, GROUP], U8, name="routed_scales", align_bytes=64)
+            difference[g] = ring.tile([P, CHUNKS, GROUP], F32, name="difference")
+
+        def mix_limbs(g, a):
+            tokens = slice(a * P, (a + 1) * P)
+            bank = banks.tile([P, CHUNKS, P], F32, tag="bank")
+            for c in range(CHUNKS):
+                nc.tensor.matmul(
+                    out=bank[:, c, :],
+                    lhsT=projected[g][:, a, c * P : (c + 1) * P],
+                    rhs=mixer_flat,
+                    start=True,
+                    stop=True,
+                )
+            nc.scalar.copy(out=routed_grouped[g][:, tokens, :], in_=bank[:].rearrange("p c r -> p r c"))
+            return bank
+
+        def keep_routed(g, a, bank):
+            tokens = slice(a * P, (a + 1) * P)
+            quantise(routed_grouped[g][:, tokens, :], routed_codes[g][:, tokens], routed_scales[g][:, tokens])
+            nc.vector.tensor_tensor(
+                out=difference[g][:, :, tokens],
+                in0=bank[:],
+                in1=x_grouped[g][:, tokens, :].rearrange("p r c -> p c r"),
+                op=ALU.subtract,
+            )
+
+        def open_gate(g):
+            gate = ring.tile([P, CHUNKS, GROUP], F32)
+            update[g] = ring.tile([P, CHUNKS, GROUP], F32, name="update")
+            for c in range(CHUNKS):
+                features = slice(c * P, (c + 1) * P)
+                bank = banks.tile([P, GROUP], F32, tag="bank")
+                nc.tensor.matmul_mx(
+                    out=bank[:],
+                    lhsT=gate_codes[:, 0, features].bitcast(FP8X4),
+                    lhsT_scale=gate_scales[:, 0, features],
+                    rhs=x_codes[g][:].bitcast(FP8X4),
+                    rhs_scale=x_scales[g][:],
+                    start=True,
+                    stop=False,
+                )
+                nc.tensor.matmul_mx(
+                    out=bank[:],
+                    lhsT=gate_codes[:, 1, features].bitcast(FP8X4),
+                    lhsT_scale=gate_scales[:, 1, features],
+                    rhs=routed_codes[g][:].bitcast(FP8X4),
+                    rhs_scale=routed_scales[g][:],
+                    start=False,
+                    stop=True,
+                )
+                nc.scalar.activation(
+                    out=gate[:, c, :], in_=bank[:], func=ACT.Sigmoid, bias=bias_gate[:, c : c + 1], scale=1.0
+                )
+                nc.gpsimd.tensor_tensor(
+                    out=update[g][:, c, :], in0=gate[:, c, :], in1=difference[g][:, c, :], op=ALU.mult
+                )
+
+        def blend(g, a):
+            tokens = slice(a * P, (a + 1) * P)
+            n = g * GROUP_TILES + a
+            bank = banks.tile([P, CHUNKS, P], F32, tag="bank")
+            for c in range(CHUNKS):
+                nc.tensor.transpose(bank[:, c, :], update[g][:, c, tokens], identity[:])
+            result = ring.tile([P, FEATURES], F32, name="result", bufs=4)
+            nc.vector.tensor_tensor(
+                out=result[:].rearrange("r (u p e) -> r u p e", u=2, e=2),
+                in0=bank[:].rearrange("r (u e) p -> r u p e", u=2),
+                in1=x_rows[:, n, :].rearrange("r (u p e) -> r u p e", u=2, e=2),
+                op=ALU.add,
+            )
+            nc.sync.dma_start(out=out_dram[:, n, :], in_=result[:])
+
+        transpose_x(1)
+        project(0)
+        quantise_x(1)
+        gate_grouped = keep.tile([P, 2, FEATURES, PACK], BF16, align_bytes=64)
+        gate_codes = keep.tile([P, 2, FEATURES], U32, align_bytes=64)
+        gate_scales = keep.tile([P, 2, FEATURES], U8, align_bytes=64)
+        gate_words = gate_rows[:].bitcast(F32)
+        for half in range(2):
+            transpose_rows(gate_words[:, :, half * 2 * P : (half + 1) * 2 * P], gate_grouped[:, half])
+        for half in range(2):
+            quantise(gate_grouped[:, half], gate_codes[:, half, :], gate_scales[:, half, :])
+
+        for s in range(GROUPS + 2):
+            if 1 <= s <= GROUPS:
+                open_gate(s - 1)
+            if s < GROUPS:
+                start_routed(s)
+            for a in range(GROUP_TILES):
+                if s < GROUPS:
+                    routed_bank = mix_limbs(s, a)
+                if s >= 2:
+                    blend(s - 2, a)
+                if s < GROUPS:
+                    keep_routed(s, a, routed_bank)
+            if s + 2 < GROUPS:
+                transpose_x(s + 2)
+            if s + 1 < GROUPS:
+                project(s + 1)
+            if s + 2 < GROUPS:
+                quantise_x(s + 2)

@@ -25,7 +25,6 @@ POSITIONS = P // LIMBS
 GROUP_TILES = 4
 GROUP = GROUP_TILES * P
 GROUPS = TILES // GROUP_TILES
-PAIRS = LIMBS * LIMBS
 PSUM_BANKS = 8
 
 FLOPS = 2 * ROWS * FEATURES * FEATURES + 2 * ROWS * 2 * FEATURES * FEATURES + 2 * ROWS * LIMBS * FEATURES
@@ -44,27 +43,6 @@ def tile_tpmslimbrouter_pa_t_kernel(
         banks = ctx.enter_context(tc.psum_pool(name="banks", bufs=PSUM_BANKS))
         ctx.enter_context(tc.manual_schedule())
 
-        route_rows = keep.tile([P, CHUNKS, FEATURES], BF16)
-        gate_rows = keep.tile([P, CHUNKS, 2 * FEATURES], BF16)
-        x_rows = keep.tile([P, TILES, FEATURES], BF16)
-
-        def load_x(g):
-            tiles = slice(g * GROUP_TILES, (g + 1) * GROUP_TILES)
-            nc.sync.dma_start(out=x_rows[:, tiles, :], in_=x_dram[:, tiles, :])
-
-        nc.sync.dma_start(
-            out=route_rows[:].rearrange("p (u e) k -> p u (e k)", u=2),
-            in_=W_route.rearrange("(u p e) k -> p u (e k)", u=2, p=P),
-        )
-        load_x(0)
-        load_x(1)
-        nc.sync.dma_start(
-            out=gate_rows[:].rearrange("p (u e) k -> p u (e k)", u=2),
-            in_=W_gate.rearrange("(u p e) k -> p u (e k)", u=2, p=P),
-        )
-        for g in range(2, GROUPS):
-            load_x(g)
-
         positions_bf = keep.tile([P, LIMBS, 3], BF16)
         threshold_bf = keep.tile([P, 1], BF16)
         b_route_bf = keep.tile([P, FEATURES], BF16)
@@ -80,6 +58,28 @@ def tile_tpmslimbrouter_pa_t_kernel(
             in_=b_gate.rearrange("(u p e) -> p u e", u=2, p=P),
         )
 
+        route_rows = keep.tile([P, CHUNKS, FEATURES], BF16)
+        gate_rows = keep.tile([P, CHUNKS, 2 * FEATURES], BF16)
+        x_rows = keep.tile([P, TILES, FEATURES], BF16)
+
+        def load_x(g):
+            for pair in range(GROUP_TILES // 2):
+                first = g * GROUP_TILES + 2 * pair
+                nc.sync.dma_start(out=x_rows[:, first : first + 2, :], in_=x_dram[:, first : first + 2, :])
+
+        nc.sync.dma_start(
+            out=route_rows[:].rearrange("p (u e) k -> p u (e k)", u=2),
+            in_=W_route.rearrange("(u p e) k -> p u (e k)", u=2, p=P),
+        )
+        load_x(0)
+        load_x(1)
+        nc.sync.dma_start(
+            out=gate_rows[:].rearrange("p (u e) k -> p u (e k)", u=2),
+            in_=W_gate.rearrange("(u p e) k -> p u (e k)", u=2, p=P),
+        )
+        for g in range(2, GROUPS):
+            load_x(g)
+
         identity = keep.tile([P, P], F32)
         masks.make_identity(nc, identity[:])
         bias_route = keep.tile([P, FEATURES], F32)
@@ -89,6 +89,10 @@ def tile_tpmslimbrouter_pa_t_kernel(
         )
         bias_gate = keep.tile([P, CHUNKS], F32)
         nc.gpsimd.tensor_copy(out=bias_gate[:], in_=b_gate_bf[:])
+
+        table_warmer = keep.tile([P, 1], F32)
+        nc.vector.memset(table_warmer[:], 0.0)
+        nc.scalar.activation(out=table_warmer[:], in_=table_warmer[:], func=ACT.Silu)
 
         def transpose_rows(rows_words, grouped):
             grouped_words = grouped.bitcast(F32)
@@ -111,35 +115,58 @@ def tile_tpmslimbrouter_pa_t_kernel(
                 out=codes.bitcast(FP8X4), scales=scales, in_=grouped.rearrange("p r t -> p (r t)")
             )
 
-        coords = keep.tile([P, 4, LIMBS], F32)
+        def quantise_halves(grouped, codes, scales):
+            for half in range(2):
+                columns = slice(half * 2 * P, (half + 1) * 2 * P)
+                quantise(grouped[:, columns, :], codes[:, columns], scales[:, columns])
+
+        own_limb = keep.tile([P, LIMBS], F32)
+        same_position = keep.tile([P, POSITIONS], F32)
+        same_block = keep.tile([P, POSITIONS, LIMBS], F32)
+        block_shape = [P, POSITIONS, LIMBS]
+        nc.vector.tensor_reduce(
+            out=own_limb[:], in_=identity[:].rearrange("q (b j) -> q j b", j=LIMBS), axis=AXIS_X, op=ALU.add
+        )
+        nc.vector.tensor_reduce(
+            out=same_position[:], in_=identity[:].rearrange("q (b j) -> q b j", j=LIMBS), axis=AXIS_X, op=ALU.add
+        )
+        nc.vector.tensor_copy(out=same_block[:], in_=same_position[:].unsqueeze(2).to_broadcast(block_shape))
+        minus_threshold = keep.tile([P, 1], F32)
+        nc.vector.tensor_scalar_mul(out=minus_threshold[:], in0=threshold_bf[:], scalar1=-1.0)
+
+        plane_shape = [P, 4, LIMBS]
+        coords = keep.tile(plane_shape, F32)
+        own_terms = keep.tile(plane_shape, F32)
+        own_coords = keep.tile([P, 4], F32)
+        pair_sum = keep.tile(plane_shape, F32)
         nc.vector.tensor_copy(out=coords[:, 0:3, :], in_=positions_bf[:].rearrange("p l c -> p c l"))
         nc.vector.tensor_copy(out=coords[:, 3, :], in_=positions_bf[:, :, 0])
-        pair_sum = keep.tile([P, 4, LIMBS, LIMBS], F32)
-        pair_shape = [P, 4, LIMBS, LIMBS]
         nc.vector.tensor_tensor(
-            out=pair_sum[:],
-            in0=coords[:].unsqueeze(3).to_broadcast(pair_shape),
-            in1=coords[:].unsqueeze(2).to_broadcast(pair_shape),
-            op=ALU.add,
+            out=own_terms[:], in0=coords[:], in1=own_limb[:].unsqueeze(1).to_broadcast(plane_shape), op=ALU.mult
         )
-        turns = keep.tile([P, 2, 3 * PAIRS], F32)
+        nc.vector.tensor_reduce(out=own_coords[:], in_=own_terms[:], axis=AXIS_X, op=ALU.add)
+        nc.vector.tensor_tensor(
+            out=pair_sum[:], in0=coords[:], in1=own_coords[:].unsqueeze(2).to_broadcast(plane_shape), op=ALU.add
+        )
+        angle_shape = [P, 2, 3 * LIMBS]
+        turns = keep.tile(angle_shape, F32)
         per_turn = 1.0 / (4.0 * math.pi)
         nc.vector.tensor_scalar_mul(
-            out=turns[:, 0, :], in0=pair_sum[:, 0:3].rearrange("p c i j -> p (c i j)"), scalar1=per_turn
+            out=turns[:, 0, :], in0=pair_sum[:, 0:3, :].rearrange("p c i -> p (c i)"), scalar1=per_turn
         )
         nc.vector.tensor_scalar(
             out=turns[:, 1, :],
-            in0=pair_sum[:, 1:4].rearrange("p c i j -> p (c i j)"),
+            in0=pair_sum[:, 1:4, :].rearrange("p c i -> p (c i)"),
             scalar1=per_turn,
             scalar2=0.25,
             op0=ALU.mult,
             op1=ALU.add,
         )
-        whole_int = keep.tile([P, 2, 3 * PAIRS], I32)
-        whole = keep.tile([P, 2, 3 * PAIRS], F32)
-        part = keep.tile([P, 2, 3 * PAIRS], F32)
-        flipped = keep.tile([P, 2, 3 * PAIRS], F32)
-        folded = keep.tile([P, 2, 3 * PAIRS], F32)
+        whole_int = keep.tile(angle_shape, I32)
+        whole = keep.tile(angle_shape, F32)
+        part = keep.tile(angle_shape, F32)
+        flipped = keep.tile(angle_shape, F32)
+        folded = keep.tile(angle_shape, F32)
         nc.vector.tensor_copy(out=whole_int[:], in_=turns[:])
         nc.vector.tensor_copy(out=whole[:], in_=whole_int[:])
         nc.vector.tensor_tensor(out=part[:], in0=turns[:], in1=whole[:], op=ALU.subtract)
@@ -149,27 +176,22 @@ def tile_tpmslimbrouter_pa_t_kernel(
         nc.vector.scalar_tensor_tensor(
             out=folded[:], in0=flipped[:], scalar=0.5, in1=flipped[:], op0=ALU.is_gt, op1=ALU.subtract
         )
-        waves = keep.tile([P, 2, 3, PAIRS], F32)
+        waves = keep.tile([P, 2, 3, LIMBS], F32)
         nc.scalar.activation(
-            out=waves[:].rearrange("p w c n -> p w (c n)"), in_=folded[:], func=ACT.Sin, scale=2.0 * math.pi
+            out=waves[:].rearrange("p w c i -> p w (c i)"), in_=folded[:], func=ACT.Sin, scale=2.0 * math.pi
         )
-        products = keep.tile([P, 3, PAIRS], F32)
-        gyroid = keep.tile([P, PAIRS], F32)
+        products = keep.tile([P, 3, LIMBS], F32)
+        gyroid = keep.tile([P, LIMBS], F32)
         nc.vector.tensor_tensor(out=products[:], in0=waves[:, 0], in1=waves[:, 1], op=ALU.mult)
         nc.vector.tensor_reduce(
-            out=gyroid[:], in_=products[:].rearrange("p c n -> p n c"), axis=AXIS_X, op=ALU.add
-        )
-        minus_2_threshold = keep.tile([P, 1], F32)
-        nc.vector.tensor_scalar_mul(out=minus_2_threshold[:], in0=threshold_bf[:], scalar1=-2.0)
-        own_limb = keep.tile([P, LIMBS], F32)
-        same_position = keep.tile([P, POSITIONS], F32)
-        nc.vector.tensor_reduce(
-            out=own_limb[:], in_=identity[:].rearrange("q (b j) -> q j b", j=LIMBS), axis=AXIS_X, op=ALU.add
-        )
-        nc.vector.tensor_reduce(
-            out=same_position[:], in_=identity[:].rearrange("q (b j) -> q b j", j=LIMBS), axis=AXIS_X, op=ALU.add
+            out=gyroid[:], in_=products[:].rearrange("p c i -> p i c"), axis=AXIS_X, op=ALU.add
         )
 
+        r = keep.tile([P, LIMBS], F32)
+
+        route_grouped = keep.tile([P, FEATURES, PACK], BF16, align_bytes=64)
+        route_codes = keep.tile([P, FEATURES], U32, align_bytes=64)
+        route_scales = keep.tile([P, FEATURES], U8, align_bytes=64)
         x_words = x_rows[:].bitcast(F32)
         x_grouped = {}
         x_codes = {}
@@ -182,39 +204,35 @@ def tile_tpmslimbrouter_pa_t_kernel(
         def quantise_x(g):
             x_codes[g] = ring.tile([P, GROUP], U32, name="x_codes", bufs=3, align_bytes=64)
             x_scales[g] = ring.tile([P, GROUP], U8, name="x_scales", bufs=3, align_bytes=64)
-            quantise(x_grouped[g][:], x_codes[g][:], x_scales[g][:])
+            quantise_halves(x_grouped[g][:], x_codes[g][:], x_scales[g][:])
 
-        route_grouped = keep.tile([P, FEATURES, PACK], BF16, align_bytes=64)
-        route_codes = keep.tile([P, FEATURES], U32, align_bytes=64)
-        route_scales = keep.tile([P, FEATURES], U8, align_bytes=64)
         transpose_rows(route_rows[:].bitcast(F32), route_grouped[:])
+        nc.scalar.activation(out=r[:], in_=gyroid[:], func=ACT.Tanh, bias=minus_threshold[:, 0:1], scale=1.0)
         transpose_x(0)
-        quantise(route_grouped[:], route_codes[:], route_scales[:])
-        quantise_x(0)
+        quantise_halves(route_grouped[:], route_codes[:], route_scales[:])
 
-        r = keep.tile([P, LIMBS, LIMBS], F32)
-        r_flat = r[:].rearrange("p i j -> p (i j)")
-        nc.scalar.activation(
-            out=r_flat, in_=gyroid[:], func=ACT.Sigmoid, bias=minus_2_threshold[:, 0:1], scale=2.0
+        nc.vector.tensor_scalar(out=r[:], in0=r[:], scalar1=0.5, scalar2=0.5, op0=ALU.mult, op1=ALU.add)
+        nc.vector.tensor_tensor(out=r[:], in0=r[:], in1=own_limb[:], op=ALU.max)
+        sums_bank = banks.tile([P, FEATURES], F32, tag="bank")
+        nc.tensor.matmul(
+            out=sums_bank[:, 0:LIMBS],
+            lhsT=same_block[:].rearrange("q b j -> q (b j)"),
+            rhs=r[:],
+            start=True,
+            stop=True,
         )
-        nc.vector.memset(r_flat[:, 0 : PAIRS : LIMBS + 1], 1.0)
+        quantise_x(0)
         row_sum = keep.tile([P, LIMBS], F32)
         inverse = keep.tile([P, LIMBS], F32)
-        nc.vector.tensor_reduce(out=row_sum[:], in_=r[:], axis=AXIS_X, op=ALU.add)
-        nc.vector.tensor_scalar_add(out=row_sum[:], in0=row_sum[:], scalar1=1e-6)
-        nc.vector.reciprocal(out=inverse[:], in_=row_sum[:])
-        picked = keep.tile([P, LIMBS, LIMBS], F32)
         weights = keep.tile([P, LIMBS], F32)
-        nc.vector.tensor_tensor(
-            out=picked[:], in0=r[:], in1=own_limb[:].unsqueeze(1).to_broadcast([P, LIMBS, LIMBS]), op=ALU.mult
-        )
-        nc.vector.tensor_reduce(out=weights[:], in_=picked[:], axis=AXIS_X, op=ALU.add)
-        nc.vector.tensor_tensor(out=weights[:], in0=weights[:], in1=inverse[:], op=ALU.mult)
-        mixer = keep.tile([P, POSITIONS, LIMBS], F32)
+        nc.vector.tensor_scalar_add(out=row_sum[:], in0=sums_bank[:, 0:LIMBS], scalar1=1e-6)
+        nc.vector.reciprocal(out=inverse[:], in_=row_sum[:])
+        nc.vector.tensor_tensor(out=weights[:], in0=r[:], in1=inverse[:], op=ALU.mult)
+        mixer = keep.tile(block_shape, F32)
         nc.vector.tensor_tensor(
             out=mixer[:],
-            in0=same_position[:].unsqueeze(2).to_broadcast([P, POSITIONS, LIMBS]),
-            in1=weights[:].unsqueeze(1).to_broadcast([P, POSITIONS, LIMBS]),
+            in0=same_position[:].unsqueeze(2).to_broadcast(block_shape),
+            in1=weights[:].unsqueeze(1).to_broadcast(block_shape),
             op=ALU.mult,
         )
         mixer_flat = mixer[:].rearrange("q b i -> q (b i)")
@@ -222,7 +240,6 @@ def tile_tpmslimbrouter_pa_t_kernel(
         projected = {}
         routed_codes = {}
         routed_scales = {}
-        routed_grouped = {}
         difference = {}
         update = {}
 
@@ -242,35 +259,30 @@ def tile_tpmslimbrouter_pa_t_kernel(
                 )
                 nc.vector.tensor_tensor(out=projected[g][:, a, :], in0=bank[:], in1=bias_route[:], op=ALU.add)
 
-        def start_routed(g):
-            routed_grouped[g] = ring.tile([P, GROUP, PACK], BF16, name="routed_grouped", align_bytes=64)
+        def mix_limbs(g):
+            routed_grouped = ring.tile([P, GROUP, PACK], BF16, align_bytes=64)
             routed_codes[g] = ring.tile([P, GROUP], U32, name="routed_codes", align_bytes=64)
             routed_scales[g] = ring.tile([P, GROUP], U8, name="routed_scales", align_bytes=64)
             difference[g] = ring.tile([P, CHUNKS, GROUP], F32, name="difference")
-
-        def mix_limbs(g, a):
-            tokens = slice(a * P, (a + 1) * P)
-            bank = banks.tile([P, CHUNKS, P], F32, tag="bank")
-            for c in range(CHUNKS):
-                nc.tensor.matmul(
-                    out=bank[:, c, :],
-                    lhsT=projected[g][:, a, c * P : (c + 1) * P],
-                    rhs=mixer_flat,
-                    start=True,
-                    stop=True,
+            for a in range(GROUP_TILES):
+                tokens = slice(a * P, (a + 1) * P)
+                bank = banks.tile([P, CHUNKS, P], F32, tag="bank")
+                for c in range(CHUNKS):
+                    nc.tensor.matmul(
+                        out=bank[:, c, :],
+                        lhsT=projected[g][:, a, c * P : (c + 1) * P],
+                        rhs=mixer_flat,
+                        start=True,
+                        stop=True,
+                    )
+                nc.scalar.copy(out=routed_grouped[:, tokens, :], in_=bank[:].rearrange("p c r -> p r c"))
+                quantise(routed_grouped[:, tokens, :], routed_codes[g][:, tokens], routed_scales[g][:, tokens])
+                nc.vector.tensor_tensor(
+                    out=difference[g][:, :, tokens],
+                    in0=bank[:],
+                    in1=x_grouped[g][:, tokens, :].rearrange("p r c -> p c r"),
+                    op=ALU.subtract,
                 )
-            nc.scalar.copy(out=routed_grouped[g][:, tokens, :], in_=bank[:].rearrange("p c r -> p r c"))
-            return bank
-
-        def keep_routed(g, a, bank):
-            tokens = slice(a * P, (a + 1) * P)
-            quantise(routed_grouped[g][:, tokens, :], routed_codes[g][:, tokens], routed_scales[g][:, tokens])
-            nc.vector.tensor_tensor(
-                out=difference[g][:, :, tokens],
-                in0=bank[:],
-                in1=x_grouped[g][:, tokens, :].rearrange("p r c -> p c r"),
-                op=ALU.subtract,
-            )
 
         def open_gate(g):
             gate = ring.tile([P, CHUNKS, GROUP], F32)
@@ -299,27 +311,38 @@ def tile_tpmslimbrouter_pa_t_kernel(
                 nc.scalar.activation(
                     out=gate[:, c, :], in_=bank[:], func=ACT.Sigmoid, bias=bias_gate[:, c : c + 1], scale=1.0
                 )
-                nc.gpsimd.tensor_tensor(
+                multiplier = nc.vector if (g == GROUPS - 1 and c % 2 == 1) else nc.gpsimd
+                multiplier.tensor_tensor(
                     out=update[g][:, c, :], in0=gate[:, c, :], in1=difference[g][:, c, :], op=ALU.mult
                 )
 
-        def blend(g, a):
-            tokens = slice(a * P, (a + 1) * P)
-            n = g * GROUP_TILES + a
-            bank = banks.tile([P, CHUNKS, P], F32, tag="bank")
-            for c in range(CHUNKS):
-                nc.tensor.transpose(bank[:, c, :], update[g][:, c, tokens], identity[:])
-            result = ring.tile([P, FEATURES], F32, name="result", bufs=4)
-            nc.vector.tensor_tensor(
-                out=result[:].rearrange("r (u p e) -> r u p e", u=2, e=2),
-                in0=bank[:].rearrange("r (u e) p -> r u p e", u=2),
-                in1=x_rows[:, n, :].rearrange("r (u p e) -> r u p e", u=2, e=2),
-                op=ALU.add,
-            )
-            nc.sync.dma_start(out=out_dram[:, n, :], in_=result[:])
+        def blend(g):
+            for a in range(GROUP_TILES):
+                tokens = slice(a * P, (a + 1) * P)
+                n = g * GROUP_TILES + a
+                bank = banks.tile([P, CHUNKS, P], F32, tag="bank")
+                for c in range(CHUNKS):
+                    nc.tensor.transpose(bank[:, c, :], update[g][:, c, tokens], identity[:])
+                result = ring.tile([P, FEATURES], F32, bufs=4)
+                nc.vector.tensor_tensor(
+                    out=result[:].rearrange("r (u p e) -> r u p e", u=2, e=2),
+                    in0=bank[:].rearrange("r (u e) p -> r u p e", u=2),
+                    in1=x_rows[:, n, :].rearrange("r (u p e) -> r u p e", u=2, e=2),
+                    op=ALU.add,
+                )
+                nc.sync.dma_start(out=out_dram[:, n, :], in_=result[:])
 
-        transpose_x(1)
+        def look_ahead(s):
+            if s + 2 < GROUPS:
+                transpose_x(s + 2)
+            if s + 1 < GROUPS:
+                project(s + 1)
+            if s + 2 < GROUPS:
+                quantise_x(s + 2)
+
         project(0)
+        mix_limbs(0)
+        transpose_x(1)
         quantise_x(1)
         gate_grouped = keep.tile([P, 2, FEATURES, PACK], BF16, align_bytes=64)
         gate_codes = keep.tile([P, 2, FEATURES], U32, align_bytes=64)
@@ -328,23 +351,14 @@ def tile_tpmslimbrouter_pa_t_kernel(
         for half in range(2):
             transpose_rows(gate_words[:, :, half * 2 * P : (half + 1) * 2 * P], gate_grouped[:, half])
         for half in range(2):
-            quantise(gate_grouped[:, half], gate_codes[:, half, :], gate_scales[:, half, :])
+            quantise_halves(gate_grouped[:, half], gate_codes[:, half, :], gate_scales[:, half, :])
+        look_ahead(0)
 
-        for s in range(GROUPS + 2):
-            if 1 <= s <= GROUPS:
+        for s in range(1, GROUPS + 2):
+            if s <= GROUPS:
                 open_gate(s - 1)
             if s < GROUPS:
-                start_routed(s)
-            for a in range(GROUP_TILES):
-                if s < GROUPS:
-                    routed_bank = mix_limbs(s, a)
-                if s >= 2:
-                    blend(s - 2, a)
-                if s < GROUPS:
-                    keep_routed(s, a, routed_bank)
-            if s + 2 < GROUPS:
-                transpose_x(s + 2)
-            if s + 1 < GROUPS:
-                project(s + 1)
-            if s + 2 < GROUPS:
-                quantise_x(s + 2)
+                mix_limbs(s)
+            if s >= 2:
+                blend(s - 2)
+            look_ahead(s)

@@ -82,14 +82,6 @@ def tile_tpmslimbrouter_pa_t_kernel(
 
         identity = keep.tile([P, P], F32)
         masks.make_identity(nc, identity[:])
-        bias_route = keep.tile([P, FEATURES], F32)
-        nc.gpsimd.tensor_copy(
-            out=bias_route[:].rearrange("q (u e p) -> q u e p", u=2, e=2),
-            in_=b_route_bf[:].rearrange("q (u p e) -> q u e p", u=2, e=2),
-        )
-        bias_gate = keep.tile([P, CHUNKS], F32)
-        nc.gpsimd.tensor_copy(out=bias_gate[:], in_=b_gate_bf[:])
-
         table_warmer = keep.tile([P, 1], F32)
         nc.vector.memset(table_warmer[:], 0.0)
         nc.scalar.activation(out=table_warmer[:], in_=table_warmer[:], func=ACT.Silu)
@@ -238,6 +230,7 @@ def tile_tpmslimbrouter_pa_t_kernel(
         mixer_flat = mixer[:].rearrange("q b i -> q (b i)")
 
         projected = {}
+        routed_grouped = {}
         routed_codes = {}
         routed_scales = {}
         difference = {}
@@ -257,32 +250,41 @@ def tile_tpmslimbrouter_pa_t_kernel(
                     start=True,
                     stop=True,
                 )
-                nc.vector.tensor_tensor(out=projected[g][:, a, :], in0=bank[:], in1=bias_route[:], op=ALU.add)
+                nc.vector.tensor_tensor(
+                    out=projected[g][:, a, :].rearrange("r (u e p) -> r u e p", u=2, e=2),
+                    in0=bank[:].rearrange("r (u e p) -> r u e p", u=2, e=2),
+                    in1=b_route_bf[:].rearrange("r (u p e) -> r u e p", u=2, e=2),
+                    op=ALU.add,
+                )
 
-        def mix_limbs(g):
-            routed_grouped = ring.tile([P, GROUP, PACK], BF16, align_bytes=64)
+        def start_routed(g):
+            routed_grouped[g] = ring.tile([P, GROUP, PACK], BF16, name="routed_grouped", align_bytes=64)
             routed_codes[g] = ring.tile([P, GROUP], U32, name="routed_codes", align_bytes=64)
             routed_scales[g] = ring.tile([P, GROUP], U8, name="routed_scales", align_bytes=64)
             difference[g] = ring.tile([P, CHUNKS, GROUP], F32, name="difference")
-            for a in range(GROUP_TILES):
-                tokens = slice(a * P, (a + 1) * P)
-                bank = banks.tile([P, CHUNKS, P], F32, tag="bank")
-                for c in range(CHUNKS):
-                    nc.tensor.matmul(
-                        out=bank[:, c, :],
-                        lhsT=projected[g][:, a, c * P : (c + 1) * P],
-                        rhs=mixer_flat,
-                        start=True,
-                        stop=True,
-                    )
-                nc.scalar.copy(out=routed_grouped[:, tokens, :], in_=bank[:].rearrange("p c r -> p r c"))
-                quantise(routed_grouped[:, tokens, :], routed_codes[g][:, tokens], routed_scales[g][:, tokens])
-                nc.vector.tensor_tensor(
-                    out=difference[g][:, :, tokens],
-                    in0=bank[:],
-                    in1=x_grouped[g][:, tokens, :].rearrange("p r c -> p c r"),
-                    op=ALU.subtract,
+
+        def mix_limbs(g, a):
+            tokens = slice(a * P, (a + 1) * P)
+            bank = banks.tile([P, CHUNKS, P], F32, tag="bank")
+            for c in range(CHUNKS):
+                nc.tensor.matmul(
+                    out=bank[:, c, :],
+                    lhsT=projected[g][:, a, c * P : (c + 1) * P],
+                    rhs=mixer_flat,
+                    start=True,
+                    stop=True,
                 )
+            nc.scalar.copy(out=routed_grouped[g][:, tokens, :], in_=bank[:].rearrange("p c r -> p r c"))
+            return bank
+
+        def subtract_x(g, a, bank):
+            tokens = slice(a * P, (a + 1) * P)
+            nc.vector.tensor_tensor(
+                out=difference[g][:, :, tokens],
+                in0=bank[:],
+                in1=x_grouped[g][:, tokens, :].rearrange("p r c -> p c r"),
+                op=ALU.subtract,
+            )
 
         def open_gate(g):
             gate = ring.tile([P, CHUNKS, GROUP], F32)
@@ -309,41 +311,51 @@ def tile_tpmslimbrouter_pa_t_kernel(
                     stop=True,
                 )
                 nc.scalar.activation(
-                    out=gate[:, c, :], in_=bank[:], func=ACT.Sigmoid, bias=bias_gate[:, c : c + 1], scale=1.0
+                    out=gate[:, c, :], in_=bank[:], func=ACT.Sigmoid, bias=b_gate_bf[:, c : c + 1], scale=1.0
                 )
-                multiplier = nc.vector if (g == GROUPS - 1 and c % 2 == 1) else nc.gpsimd
-                multiplier.tensor_tensor(
+                nc.gpsimd.tensor_tensor(
                     out=update[g][:, c, :], in0=gate[:, c, :], in1=difference[g][:, c, :], op=ALU.mult
                 )
 
-        def blend(g):
+        def blend(g, a):
+            tokens = slice(a * P, (a + 1) * P)
+            n = g * GROUP_TILES + a
+            bank = banks.tile([P, CHUNKS, P], F32, tag="bank")
+            for c in range(CHUNKS):
+                nc.tensor.transpose(bank[:, c, :], update[g][:, c, tokens], identity[:])
+            result = ring.tile([P, FEATURES], F32, bufs=4)
+            nc.vector.tensor_tensor(
+                out=result[:].rearrange("r (u p e) -> r u p e", u=2, e=2),
+                in0=bank[:].rearrange("r (u e) p -> r u p e", u=2),
+                in1=x_rows[:, n, :].rearrange("r (u p e) -> r u p e", u=2, e=2),
+                op=ALU.add,
+            )
+            nc.sync.dma_start(out=out_dram[:, n, :], in_=result[:])
+
+        def mix_and_blend(s):
+            if s < GROUPS:
+                start_routed(s)
             for a in range(GROUP_TILES):
-                tokens = slice(a * P, (a + 1) * P)
-                n = g * GROUP_TILES + a
-                bank = banks.tile([P, CHUNKS, P], F32, tag="bank")
-                for c in range(CHUNKS):
-                    nc.tensor.transpose(bank[:, c, :], update[g][:, c, tokens], identity[:])
-                result = ring.tile([P, FEATURES], F32, bufs=4)
-                nc.vector.tensor_tensor(
-                    out=result[:].rearrange("r (u p e) -> r u p e", u=2, e=2),
-                    in0=bank[:].rearrange("r (u e) p -> r u p e", u=2),
-                    in1=x_rows[:, n, :].rearrange("r (u p e) -> r u p e", u=2, e=2),
-                    op=ALU.add,
-                )
-                nc.sync.dma_start(out=out_dram[:, n, :], in_=result[:])
+                if s < GROUPS:
+                    routed_bank = mix_limbs(s, a)
+                if s < GROUPS and a == GROUP_TILES - 1:
+                    quantise(routed_grouped[s][:], routed_codes[s][:], routed_scales[s][:])
+                if s >= 2:
+                    blend(s - 2, a)
+                if s < GROUPS:
+                    subtract_x(s, a, routed_bank)
 
         def look_ahead(s):
             if s + 2 < GROUPS:
                 transpose_x(s + 2)
+                quantise_x(s + 2)
             if s + 1 < GROUPS:
                 project(s + 1)
-            if s + 2 < GROUPS:
-                quantise_x(s + 2)
 
         project(0)
-        mix_limbs(0)
         transpose_x(1)
         quantise_x(1)
+        mix_and_blend(0)
         gate_grouped = keep.tile([P, 2, FEATURES, PACK], BF16, align_bytes=64)
         gate_codes = keep.tile([P, 2, FEATURES], U32, align_bytes=64)
         gate_scales = keep.tile([P, 2, FEATURES], U8, align_bytes=64)
@@ -357,8 +369,5 @@ def tile_tpmslimbrouter_pa_t_kernel(
         for s in range(1, GROUPS + 2):
             if s <= GROUPS:
                 open_gate(s - 1)
-            if s < GROUPS:
-                mix_limbs(s)
-            if s >= 2:
-                blend(s - 2)
+            mix_and_blend(s)
             look_ahead(s)

@@ -26,6 +26,7 @@ GROUP_TILES = 4
 GROUP = GROUP_TILES * P
 GROUPS = TILES // GROUP_TILES
 PSUM_BANKS = 8
+BANK_COLUMNS = 2 * P
 
 FLOPS = 2 * ROWS * FEATURES * FEATURES + 2 * ROWS * 2 * FEATURES * FEATURES + 2 * ROWS * LIMBS * FEATURES
 
@@ -52,19 +53,13 @@ def tile_tpmslimbrouter_pa_t_kernel(
             in_=limb_positions.rearrange("l c -> (l c)").partition_broadcast(P),
         )
         nc.scalar.dma_start(out=threshold_bf[:], in_=channel_threshold.partition_broadcast(P))
-        nc.scalar.dma_start(out=b_route_bf[:], in_=b_route.partition_broadcast(P))
-        nc.scalar.dma_start(
-            out=b_gate_bf[:].rearrange("p (u e) -> p u e", u=2),
-            in_=b_gate.rearrange("(u p e) -> p u e", u=2, p=P),
-        )
 
         route_rows = keep.tile([P, CHUNKS, FEATURES], BF16)
         gate_rows = keep.tile([P, CHUNKS, 2 * FEATURES], BF16)
         x_rows = keep.tile([P, TILES, FEATURES], BF16)
 
         def load_x(g):
-            for pair in range(GROUP_TILES // 2):
-                first = g * GROUP_TILES + 2 * pair
+            for first in range(g * GROUP_TILES, (g + 1) * GROUP_TILES, 2):
                 nc.sync.dma_start(out=x_rows[:, first : first + 2, :], in_=x_dram[:, first : first + 2, :])
 
         nc.sync.dma_start(
@@ -72,12 +67,18 @@ def tile_tpmslimbrouter_pa_t_kernel(
             in_=W_route.rearrange("(u p e) k -> p u (e k)", u=2, p=P),
         )
         load_x(0)
+        nc.sync.dma_start(out=b_route_bf[:], in_=b_route.partition_broadcast(P))
         load_x(1)
         nc.sync.dma_start(
             out=gate_rows[:].rearrange("p (u e) k -> p u (e k)", u=2),
             in_=W_gate.rearrange("(u p e) k -> p u (e k)", u=2, p=P),
         )
-        for g in range(2, GROUPS):
+        load_x(2)
+        nc.sync.dma_start(
+            out=b_gate_bf[:].rearrange("p (u e) -> p u e", u=2),
+            in_=b_gate.rearrange("(u p e) -> p u e", u=2, p=P),
+        )
+        for g in range(3, GROUPS):
             load_x(g)
 
         identity = keep.tile([P, P], F32)
@@ -86,33 +87,26 @@ def tile_tpmslimbrouter_pa_t_kernel(
         nc.vector.memset(table_warmer[:], 0.0)
         nc.scalar.activation(out=table_warmer[:], in_=table_warmer[:], func=ACT.Silu)
 
-        def transpose_rows(rows_words, grouped):
-            grouped_words = grouped.bitcast(F32)
-            for half in range(2):
-                bank = banks.tile([P, 2, 2, P], F32, tag="bank")
-                for i in range(2):
-                    for u in range(2):
-                        nc.tensor.transpose(
-                            bank[:, i, u, :], rows_words[:, 2 * half + i, u * P : (u + 1) * P], identity[:]
-                        )
-                nc.scalar.copy(
-                    out=grouped_words[:, half * 2 * P : (half + 1) * 2 * P, :].rearrange(
-                        "p (i r) u -> p i r u", i=2
-                    ),
-                    in_=bank[:].rearrange("p i u r -> p i r u"),
-                )
+        def transpose_bank(rows_words, grouped):
+            bank = banks.tile([P, 2, 2, P], F32, tag="bank")
+            for i in range(2):
+                for u in range(2):
+                    nc.tensor.transpose(bank[:, i, u, :], rows_words[:, i, u * P : (u + 1) * P], identity[:])
+            nc.scalar.copy(
+                out=grouped.bitcast(F32).rearrange("p (i r) u -> p i r u", i=2),
+                in_=bank[:].rearrange("p i u r -> p i r u"),
+            )
 
         def quantise(grouped, codes, scales):
             nc.vector.quantize_mx(
                 out=codes.bitcast(FP8X4), scales=scales, in_=grouped.rearrange("p r t -> p (r t)")
             )
 
-        def quantise_halves(grouped, codes, scales):
-            for half in range(2):
-                columns = slice(half * 2 * P, (half + 1) * 2 * P)
-                quantise(grouped[:, columns, :], codes[:, columns], scales[:, columns])
+        def bank_columns(half):
+            return slice(half * BANK_COLUMNS, (half + 1) * BANK_COLUMNS)
 
         own_limb = keep.tile([P, LIMBS], F32)
+        own_sign = keep.tile([P, LIMBS], F32)
         same_position = keep.tile([P, POSITIONS], F32)
         same_block = keep.tile([P, POSITIONS, LIMBS], F32)
         block_shape = [P, POSITIONS, LIMBS]
@@ -122,46 +116,43 @@ def tile_tpmslimbrouter_pa_t_kernel(
         nc.vector.tensor_reduce(
             out=same_position[:], in_=identity[:].rearrange("q (b j) -> q b j", j=LIMBS), axis=AXIS_X, op=ALU.add
         )
-        nc.vector.tensor_copy(out=same_block[:], in_=same_position[:].unsqueeze(2).to_broadcast(block_shape))
-        minus_threshold = keep.tile([P, 1], F32)
-        nc.vector.tensor_scalar_mul(out=minus_threshold[:], in0=threshold_bf[:], scalar1=-1.0)
-
-        plane_shape = [P, 4, LIMBS]
-        coords = keep.tile(plane_shape, F32)
-        own_terms = keep.tile(plane_shape, F32)
-        own_coords = keep.tile([P, 4], F32)
-        pair_sum = keep.tile(plane_shape, F32)
-        nc.vector.tensor_copy(out=coords[:, 0:3, :], in_=positions_bf[:].rearrange("p l c -> p c l"))
-        nc.vector.tensor_copy(out=coords[:, 3, :], in_=positions_bf[:, :, 0])
-        nc.vector.tensor_tensor(
-            out=own_terms[:], in0=coords[:], in1=own_limb[:].unsqueeze(1).to_broadcast(plane_shape), op=ALU.mult
-        )
-        nc.vector.tensor_reduce(out=own_coords[:], in_=own_terms[:], axis=AXIS_X, op=ALU.add)
-        nc.vector.tensor_tensor(
-            out=pair_sum[:], in0=coords[:], in1=own_coords[:].unsqueeze(2).to_broadcast(plane_shape), op=ALU.add
-        )
-        angle_shape = [P, 2, 3 * LIMBS]
-        turns = keep.tile(angle_shape, F32)
-        per_turn = 1.0 / (4.0 * math.pi)
-        nc.vector.tensor_scalar_mul(
-            out=turns[:, 0, :], in0=pair_sum[:, 0:3, :].rearrange("p c i -> p (c i)"), scalar1=per_turn
-        )
         nc.vector.tensor_scalar(
-            out=turns[:, 1, :],
-            in0=pair_sum[:, 1:4, :].rearrange("p c i -> p (c i)"),
-            scalar1=per_turn,
-            scalar2=0.25,
+            out=own_sign[:], in0=own_limb[:], scalar1=2.0, scalar2=-1.0, op0=ALU.mult, op1=ALU.add
+        )
+        nc.vector.tensor_copy(out=same_block[:], in_=same_position[:].unsqueeze(2).to_broadcast(block_shape))
+
+        plane_shape = [P, 3, LIMBS]
+        positions = positions_bf[:].rearrange("p l c -> p c l")
+        per_turn = 1.0 / (4.0 * math.pi)
+        own_terms = keep.tile(plane_shape, F32)
+        own_turns = keep.tile([P, 3], F32)
+        turns = keep.tile([P, 2, 3, LIMBS], F32)
+        nc.vector.scalar_tensor_tensor(
+            out=own_terms[:],
+            in0=positions,
+            scalar=per_turn,
+            in1=own_limb[:].unsqueeze(1).to_broadcast(plane_shape),
+            op0=ALU.mult,
+            op1=ALU.mult,
+        )
+        nc.vector.tensor_reduce(out=own_turns[:], in_=own_terms[:], axis=AXIS_X, op=ALU.add)
+        nc.vector.scalar_tensor_tensor(
+            out=turns[:, 0],
+            in0=positions,
+            scalar=per_turn,
+            in1=own_turns[:].unsqueeze(2).to_broadcast(plane_shape),
             op0=ALU.mult,
             op1=ALU.add,
         )
-        whole_int = keep.tile(angle_shape, I32)
-        whole = keep.tile(angle_shape, F32)
+        nc.vector.tensor_scalar_add(out=turns[:, 1], in0=turns[:, 0], scalar1=0.25)
+        angle_shape = [P, 2 * 3 * LIMBS]
+        turns_flat = turns[:].rearrange("p w c i -> p (w c i)")
+        whole = keep.tile(angle_shape, I32)
         part = keep.tile(angle_shape, F32)
         flipped = keep.tile(angle_shape, F32)
         folded = keep.tile(angle_shape, F32)
-        nc.vector.tensor_copy(out=whole_int[:], in_=turns[:])
-        nc.vector.tensor_copy(out=whole[:], in_=whole_int[:])
-        nc.vector.tensor_tensor(out=part[:], in0=turns[:], in1=whole[:], op=ALU.subtract)
+        nc.vector.tensor_copy(out=whole[:], in_=turns_flat)
+        nc.vector.tensor_tensor(out=part[:], in0=turns_flat, in1=whole[:], op=ALU.subtract)
         nc.vector.scalar_tensor_tensor(
             out=flipped[:], in0=part[:], scalar=0.5, in1=part[:], op0=ALU.is_gt, op1=ALU.subtract
         )
@@ -170,56 +161,71 @@ def tile_tpmslimbrouter_pa_t_kernel(
         )
         waves = keep.tile([P, 2, 3, LIMBS], F32)
         nc.scalar.activation(
-            out=waves[:].rearrange("p w c i -> p w (c i)"), in_=folded[:], func=ACT.Sin, scale=2.0 * math.pi
+            out=waves[:].rearrange("p w c i -> p (w c i)"), in_=folded[:], func=ACT.Sin, scale=2.0 * math.pi
         )
-        products = keep.tile([P, 3, LIMBS], F32)
+        products = keep.tile(plane_shape, F32)
         gyroid = keep.tile([P, LIMBS], F32)
-        nc.vector.tensor_tensor(out=products[:], in0=waves[:, 0], in1=waves[:, 1], op=ALU.mult)
+        minus_threshold = keep.tile([P, 1], F32)
+        nc.vector.tensor_tensor(out=products[:, 0:2], in0=waves[:, 0, 0:2], in1=waves[:, 1, 1:3], op=ALU.mult)
+        nc.vector.tensor_tensor(out=products[:, 2], in0=waves[:, 0, 2], in1=waves[:, 1, 0], op=ALU.mult)
+        nc.vector.tensor_scalar_mul(out=minus_threshold[:], in0=threshold_bf[:], scalar1=-1.0)
         nc.vector.tensor_reduce(
             out=gyroid[:], in_=products[:].rearrange("p c i -> p i c"), axis=AXIS_X, op=ALU.add
         )
 
-        r = keep.tile([P, LIMBS], F32)
-
         route_grouped = keep.tile([P, FEATURES, PACK], BF16, align_bytes=64)
         route_codes = keep.tile([P, FEATURES], U32, align_bytes=64)
         route_scales = keep.tile([P, FEATURES], U8, align_bytes=64)
+        route_words = route_rows[:].bitcast(F32)
         x_words = x_rows[:].bitcast(F32)
         x_grouped = {}
         x_codes = {}
         x_scales = {}
 
+        def transpose_route(half):
+            transpose_bank(route_words[:, 2 * half : 2 * half + 2, :], route_grouped[:, bank_columns(half), :])
+
+        def quantise_route(half):
+            columns = bank_columns(half)
+            quantise(route_grouped[:, columns, :], route_codes[:, columns], route_scales[:, columns])
+
         def transpose_x(g):
             x_grouped[g] = ring.tile([P, GROUP, PACK], BF16, name="x_grouped", bufs=3, align_bytes=64)
-            transpose_rows(x_words[:, g * GROUP_TILES : (g + 1) * GROUP_TILES, :], x_grouped[g][:])
+            for half in range(GROUP_TILES // 2):
+                first = g * GROUP_TILES + 2 * half
+                transpose_bank(x_words[:, first : first + 2, :], x_grouped[g][:, bank_columns(half), :])
 
         def quantise_x(g):
             x_codes[g] = ring.tile([P, GROUP], U32, name="x_codes", bufs=3, align_bytes=64)
             x_scales[g] = ring.tile([P, GROUP], U8, name="x_scales", bufs=3, align_bytes=64)
-            quantise_halves(x_grouped[g][:], x_codes[g][:], x_scales[g][:])
+            for half in range(GROUP_TILES // 2):
+                columns = bank_columns(half)
+                quantise(x_grouped[g][:, columns, :], x_codes[g][:, columns], x_scales[g][:, columns])
 
-        transpose_rows(route_rows[:].bitcast(F32), route_grouped[:])
-        nc.scalar.activation(out=r[:], in_=gyroid[:], func=ACT.Tanh, bias=minus_threshold[:, 0:1], scale=1.0)
+        tanh = keep.tile([P, LIMBS], F32)
+        transpose_route(0)
+        nc.scalar.activation(out=tanh[:], in_=gyroid[:], func=ACT.Tanh, bias=minus_threshold[:, 0:1], scale=1.0)
+        transpose_route(1)
         transpose_x(0)
-        quantise_halves(route_grouped[:], route_codes[:], route_scales[:])
-
-        nc.vector.tensor_scalar(out=r[:], in0=r[:], scalar1=0.5, scalar2=0.5, op0=ALU.mult, op1=ALU.add)
-        nc.vector.tensor_tensor(out=r[:], in0=r[:], in1=own_limb[:], op=ALU.max)
+        quantise_route(0)
+        nc.vector.tensor_tensor(out=tanh[:], in0=tanh[:], in1=own_sign[:], op=ALU.max)
+        quantise_route(1)
         sums_bank = banks.tile([P, FEATURES], F32, tag="bank")
         nc.tensor.matmul(
             out=sums_bank[:, 0:LIMBS],
             lhsT=same_block[:].rearrange("q b j -> q (b j)"),
-            rhs=r[:],
+            rhs=tanh[:],
             start=True,
             stop=True,
         )
-        quantise_x(0)
         row_sum = keep.tile([P, LIMBS], F32)
         inverse = keep.tile([P, LIMBS], F32)
         weights = keep.tile([P, LIMBS], F32)
-        nc.vector.tensor_scalar_add(out=row_sum[:], in0=sums_bank[:, 0:LIMBS], scalar1=1e-6)
+        nc.vector.tensor_scalar_add(out=row_sum[:], in0=sums_bank[:, 0:LIMBS], scalar1=LIMBS + 2e-6)
         nc.vector.reciprocal(out=inverse[:], in_=row_sum[:])
-        nc.vector.tensor_tensor(out=weights[:], in0=r[:], in1=inverse[:], op=ALU.mult)
+        nc.vector.scalar_tensor_tensor(
+            out=weights[:], in0=tanh[:], scalar=1.0, in1=inverse[:], op0=ALU.add, op1=ALU.mult
+        )
         mixer = keep.tile(block_shape, F32)
         nc.vector.tensor_tensor(
             out=mixer[:],
@@ -228,12 +234,14 @@ def tile_tpmslimbrouter_pa_t_kernel(
             op=ALU.mult,
         )
         mixer_flat = mixer[:].rearrange("q b i -> q (b i)")
+        quantise_x(0)
 
         projected = {}
         routed_grouped = {}
         routed_codes = {}
         routed_scales = {}
         difference = {}
+        gate = {}
         update = {}
 
         def project(g):
@@ -286,35 +294,47 @@ def tile_tpmslimbrouter_pa_t_kernel(
                 op=ALU.subtract,
             )
 
-        def open_gate(g):
-            gate = ring.tile([P, CHUNKS, GROUP], F32)
+        def quantise_routed(g, tokens):
+            quantise(routed_grouped[g][:, tokens, :], routed_codes[g][:, tokens], routed_scales[g][:, tokens])
+
+        def start_gate(g):
+            gate[g] = ring.tile([P, CHUNKS, GROUP], F32, name="gate")
             update[g] = ring.tile([P, CHUNKS, GROUP], F32, name="update")
+
+        def open_gate(g, tokens, multiplier):
             for c in range(CHUNKS):
                 features = slice(c * P, (c + 1) * P)
                 bank = banks.tile([P, GROUP], F32, tag="bank")
                 nc.tensor.matmul_mx(
-                    out=bank[:],
+                    out=bank[:, tokens],
                     lhsT=gate_codes[:, 0, features].bitcast(FP8X4),
                     lhsT_scale=gate_scales[:, 0, features],
-                    rhs=x_codes[g][:].bitcast(FP8X4),
-                    rhs_scale=x_scales[g][:],
+                    rhs=x_codes[g][:, tokens].bitcast(FP8X4),
+                    rhs_scale=x_scales[g][:, tokens],
                     start=True,
                     stop=False,
                 )
                 nc.tensor.matmul_mx(
-                    out=bank[:],
+                    out=bank[:, tokens],
                     lhsT=gate_codes[:, 1, features].bitcast(FP8X4),
                     lhsT_scale=gate_scales[:, 1, features],
-                    rhs=routed_codes[g][:].bitcast(FP8X4),
-                    rhs_scale=routed_scales[g][:],
+                    rhs=routed_codes[g][:, tokens].bitcast(FP8X4),
+                    rhs_scale=routed_scales[g][:, tokens],
                     start=False,
                     stop=True,
                 )
                 nc.scalar.activation(
-                    out=gate[:, c, :], in_=bank[:], func=ACT.Sigmoid, bias=b_gate_bf[:, c : c + 1], scale=1.0
+                    out=gate[g][:, c, tokens],
+                    in_=bank[:, tokens],
+                    func=ACT.Sigmoid,
+                    bias=b_gate_bf[:, c : c + 1],
+                    scale=1.0,
                 )
-                nc.gpsimd.tensor_tensor(
-                    out=update[g][:, c, :], in0=gate[:, c, :], in1=difference[g][:, c, :], op=ALU.mult
+                multiplier.tensor_tensor(
+                    out=update[g][:, c, tokens],
+                    in0=gate[g][:, c, tokens],
+                    in1=difference[g][:, c, tokens],
+                    op=ALU.mult,
                 )
 
         def blend(g, a):
@@ -333,17 +353,14 @@ def tile_tpmslimbrouter_pa_t_kernel(
             nc.sync.dma_start(out=out_dram[:, n, :], in_=result[:])
 
         def mix_and_blend(s):
-            if s < GROUPS:
-                start_routed(s)
+            start_routed(s)
             for a in range(GROUP_TILES):
-                if s < GROUPS:
-                    routed_bank = mix_limbs(s, a)
-                if s < GROUPS and a == GROUP_TILES - 1:
-                    quantise(routed_grouped[s][:], routed_codes[s][:], routed_scales[s][:])
+                routed_bank = mix_limbs(s, a)
+                if a == GROUP_TILES - 1:
+                    quantise_routed(s, slice(0, GROUP))
                 if s >= 2:
                     blend(s - 2, a)
-                if s < GROUPS:
-                    subtract_x(s, a, routed_bank)
+                subtract_x(s, a, routed_bank)
 
         def look_ahead(s):
             if s + 2 < GROUPS:
@@ -352,22 +369,75 @@ def tile_tpmslimbrouter_pa_t_kernel(
             if s + 1 < GROUPS:
                 project(s + 1)
 
-        project(0)
-        transpose_x(1)
-        quantise_x(1)
-        mix_and_blend(0)
         gate_grouped = keep.tile([P, 2, FEATURES, PACK], BF16, align_bytes=64)
         gate_codes = keep.tile([P, 2, FEATURES], U32, align_bytes=64)
         gate_scales = keep.tile([P, 2, FEATURES], U8, align_bytes=64)
         gate_words = gate_rows[:].bitcast(F32)
-        for half in range(2):
-            transpose_rows(gate_words[:, :, half * 2 * P : (half + 1) * 2 * P], gate_grouped[:, half])
-        for half in range(2):
-            quantise_halves(gate_grouped[:, half], gate_codes[:, half, :], gate_scales[:, half, :])
-        look_ahead(0)
 
-        for s in range(1, GROUPS + 2):
-            if s <= GROUPS:
-                open_gate(s - 1)
+        def transpose_gate(side):
+            words = gate_words[:, :, side * 2 * P : (side + 1) * 2 * P]
+            for half in range(2):
+                transpose_bank(words[:, 2 * half : 2 * half + 2, :], gate_grouped[:, side, bank_columns(half), :])
+
+        def quantise_gate(side):
+            for half in range(2):
+                columns = bank_columns(half)
+                quantise(
+                    gate_grouped[:, side, columns, :], gate_codes[:, side, columns], gate_scales[:, side, columns]
+                )
+
+        project(0)
+        transpose_x(1)
+        quantise_x(1)
+        start_routed(0)
+        between = [
+            (lambda: transpose_gate(0), lambda: quantise_gate(0)),
+            (lambda: transpose_gate(1), lambda: quantise_gate(1)),
+            (lambda: transpose_x(2), lambda: quantise_x(2)),
+        ]
+        for a in range(GROUP_TILES):
+            routed_bank = mix_limbs(0, a)
+            if a < len(between):
+                between[a][0]()
+                subtract_x(0, a, routed_bank)
+                between[a][1]()
+            else:
+                quantise_routed(0, slice(0, GROUP))
+                subtract_x(0, a, routed_bank)
+        project(1)
+
+        for s in range(1, GROUPS - 1):
+            start_gate(s - 1)
+            open_gate(s - 1, slice(0, GROUP), nc.gpsimd)
             mix_and_blend(s)
             look_ahead(s)
+
+        last = GROUPS - 1
+        first_half, second_half = slice(0, GROUP // 2), slice(GROUP // 2, GROUP)
+        start_gate(last - 1)
+        open_gate(last - 1, slice(0, GROUP), nc.gpsimd)
+        start_routed(last)
+        start_gate(last)
+        ways_back = [
+            [(last - 2, 0), (last - 2, 1)],
+            [(last - 2, 2), (last - 2, 3)],
+            [(last - 1, 0), (last - 1, 1)],
+            [],
+        ]
+        for a in range(GROUP_TILES):
+            routed_bank = mix_limbs(last, a)
+            if a == 1:
+                quantise_routed(last, first_half)
+            if a == 3:
+                quantise_routed(last, second_half)
+            for back in ways_back[a][:1]:
+                blend(*back)
+            subtract_x(last, a, routed_bank)
+            for back in ways_back[a][1:]:
+                blend(*back)
+        open_gate(last, first_half, nc.gpsimd)
+        blend(last - 1, 2)
+        blend(last - 1, 3)
+        open_gate(last, second_half, nc.vector)
+        for a in range(GROUP_TILES):
+            blend(last, a)

@@ -48,11 +48,11 @@ def tile_tpmslimbrouter_pa_t_kernel(
         threshold_bf = keep.tile([P, 1], BF16)
         b_route_bf = keep.tile([P, FEATURES], BF16)
         b_gate_bf = keep.tile([P, CHUNKS], BF16)
-        nc.scalar.dma_start(
+        nc.sync.dma_start(
             out=positions_bf[:].rearrange("p l c -> p (l c)"),
             in_=limb_positions.rearrange("l c -> (l c)").partition_broadcast(P),
         )
-        nc.scalar.dma_start(out=threshold_bf[:], in_=channel_threshold.partition_broadcast(P))
+        nc.sync.dma_start(out=threshold_bf[:], in_=channel_threshold.partition_broadcast(P))
 
         route_rows = keep.tile([P, CHUNKS, FEATURES], BF16)
         gate_rows = keep.tile([P, CHUNKS, 2 * FEATURES], BF16)
@@ -87,15 +87,23 @@ def tile_tpmslimbrouter_pa_t_kernel(
         nc.vector.memset(table_warmer[:], 0.0)
         nc.scalar.activation(out=table_warmer[:], in_=table_warmer[:], func=ACT.Silu)
 
-        def transpose_bank(rows_words, grouped):
-            bank = banks.tile([P, 2, 2, P], F32, tag="bank")
-            for i in range(2):
-                for u in range(2):
-                    nc.tensor.transpose(bank[:, i, u, :], rows_words[:, i, u * P : (u + 1) * P], identity[:])
-            nc.scalar.copy(
-                out=grouped.bitcast(F32).rearrange("p (i r) u -> p i r u", i=2),
-                in_=bank[:].rearrange("p i u r -> p i r u"),
-            )
+        def transpose_rows(rows_words, grouped):
+            bank = banks.tile([P, 2, 2, P], F32, name="rows_bank", tag="bank")
+
+            def transpose(k):
+                i, u = divmod(k, 2)
+                nc.tensor.transpose(bank[:, i, u, :], rows_words[:, i, u * P : (u + 1) * P], identity[:])
+                if k == 3:
+                    nc.scalar.copy(
+                        out=grouped.bitcast(F32).rearrange("p (i r) u -> p i r u", i=2),
+                        in_=bank[:].rearrange("p i u r -> p i r u"),
+                    )
+
+            return transpose
+
+        def run(job):
+            for k in range(4):
+                job(k)
 
         def quantise(grouped, codes, scales):
             nc.vector.quantize_mx(
@@ -159,6 +167,42 @@ def tile_tpmslimbrouter_pa_t_kernel(
         nc.vector.scalar_tensor_tensor(
             out=folded[:], in0=flipped[:], scalar=0.5, in1=flipped[:], op0=ALU.is_gt, op1=ALU.subtract
         )
+        route_grouped = keep.tile([P, FEATURES, PACK], BF16, align_bytes=64)
+        route_codes = keep.tile([P, FEATURES], U32, align_bytes=64)
+        route_scales = keep.tile([P, FEATURES], U8, align_bytes=64)
+        route_words = route_rows[:].bitcast(F32)
+        x_words = x_rows[:].bitcast(F32)
+        x_grouped = {}
+        x_codes = {}
+        x_scales = {}
+
+        def transpose_route(half):
+            return transpose_rows(
+                route_words[:, 2 * half : 2 * half + 2, :], route_grouped[:, bank_columns(half), :]
+            )
+
+        def quantise_route(half):
+            columns = bank_columns(half)
+            quantise(route_grouped[:, columns, :], route_codes[:, columns], route_scales[:, columns])
+
+        def start_x(g):
+            x_grouped[g] = ring.tile([P, GROUP, PACK], BF16, name="x_grouped", bufs=3, align_bytes=64)
+            x_codes[g] = ring.tile([P, GROUP], U32, name="x_codes", bufs=3, align_bytes=64)
+            x_scales[g] = ring.tile([P, GROUP], U8, name="x_scales", bufs=3, align_bytes=64)
+
+        def transpose_x(g, half):
+            first = g * GROUP_TILES + 2 * half
+            return transpose_rows(x_words[:, first : first + 2, :], x_grouped[g][:, bank_columns(half), :])
+
+        def quantise_x(g, half):
+            columns = bank_columns(half)
+            quantise(x_grouped[g][:, columns, :], x_codes[g][:, columns], x_scales[g][:, columns])
+
+        start_x(0)
+        start_x(1)
+        run(transpose_route(0))
+        run(transpose_route(1))
+        quantise_route(0)
         waves = keep.tile([P, 2, 3, LIMBS], F32)
         nc.scalar.activation(
             out=waves[:].rearrange("p w c i -> p (w c i)"), in_=folded[:], func=ACT.Sin, scale=2.0 * math.pi
@@ -172,70 +216,19 @@ def tile_tpmslimbrouter_pa_t_kernel(
         nc.vector.tensor_reduce(
             out=gyroid[:], in_=products[:].rearrange("p c i -> p i c"), axis=AXIS_X, op=ALU.add
         )
-
-        route_grouped = keep.tile([P, FEATURES, PACK], BF16, align_bytes=64)
-        route_codes = keep.tile([P, FEATURES], U32, align_bytes=64)
-        route_scales = keep.tile([P, FEATURES], U8, align_bytes=64)
-        route_words = route_rows[:].bitcast(F32)
-        x_words = x_rows[:].bitcast(F32)
-        x_grouped = {}
-        x_codes = {}
-        x_scales = {}
-
-        def transpose_route(half):
-            transpose_bank(route_words[:, 2 * half : 2 * half + 2, :], route_grouped[:, bank_columns(half), :])
-
-        def quantise_route(half):
-            columns = bank_columns(half)
-            quantise(route_grouped[:, columns, :], route_codes[:, columns], route_scales[:, columns])
-
-        def transpose_x(g):
-            x_grouped[g] = ring.tile([P, GROUP, PACK], BF16, name="x_grouped", bufs=3, align_bytes=64)
-            for half in range(GROUP_TILES // 2):
-                first = g * GROUP_TILES + 2 * half
-                transpose_bank(x_words[:, first : first + 2, :], x_grouped[g][:, bank_columns(half), :])
-
-        def quantise_x(g):
-            x_codes[g] = ring.tile([P, GROUP], U32, name="x_codes", bufs=3, align_bytes=64)
-            x_scales[g] = ring.tile([P, GROUP], U8, name="x_scales", bufs=3, align_bytes=64)
-            for half in range(GROUP_TILES // 2):
-                columns = bank_columns(half)
-                quantise(x_grouped[g][:, columns, :], x_codes[g][:, columns], x_scales[g][:, columns])
-
-        tanh = keep.tile([P, LIMBS], F32)
-        transpose_route(0)
-        nc.scalar.activation(out=tanh[:], in_=gyroid[:], func=ACT.Tanh, bias=minus_threshold[:, 0:1], scale=1.0)
-        transpose_route(1)
-        transpose_x(0)
-        quantise_route(0)
-        nc.vector.tensor_tensor(out=tanh[:], in0=tanh[:], in1=own_sign[:], op=ALU.max)
         quantise_route(1)
-        sums_bank = banks.tile([P, FEATURES], F32, tag="bank")
-        nc.tensor.matmul(
-            out=sums_bank[:, 0:LIMBS],
-            lhsT=same_block[:].rearrange("q b j -> q (b j)"),
-            rhs=tanh[:],
-            start=True,
-            stop=True,
-        )
-        row_sum = keep.tile([P, LIMBS], F32)
-        inverse = keep.tile([P, LIMBS], F32)
-        weights = keep.tile([P, LIMBS], F32)
-        nc.vector.tensor_scalar_add(out=row_sum[:], in0=sums_bank[:, 0:LIMBS], scalar1=LIMBS + 2e-6)
-        nc.vector.reciprocal(out=inverse[:], in_=row_sum[:])
-        nc.vector.scalar_tensor_tensor(
-            out=weights[:], in0=tanh[:], scalar=1.0, in1=inverse[:], op0=ALU.add, op1=ALU.mult
-        )
-        mixer = keep.tile(block_shape, F32)
-        nc.vector.tensor_tensor(
-            out=mixer[:],
-            in0=same_position[:].unsqueeze(2).to_broadcast(block_shape),
-            in1=weights[:].unsqueeze(1).to_broadcast(block_shape),
-            op=ALU.mult,
-        )
-        mixer_flat = mixer[:].rearrange("q b i -> q (b i)")
-        quantise_x(0)
+        run(transpose_x(0, 0))
+        run(transpose_x(0, 1))
+        tanh = keep.tile([P, LIMBS], F32)
+        nc.scalar.activation(out=tanh[:], in_=gyroid[:], func=ACT.Tanh, bias=minus_threshold[:, 0:1], scale=1.0)
+        quantise_x(0, 0)
+        nc.vector.tensor_tensor(out=tanh[:], in0=tanh[:], in1=own_sign[:], op=ALU.max)
+        quantise_x(0, 1)
+        run(transpose_x(1, 0))
+        run(transpose_x(1, 1))
 
+        mixer = keep.tile(block_shape, F32)
+        mixer_flat = mixer[:].rearrange("q b i -> q (b i)")
         projected = {}
         routed_grouped = {}
         routed_codes = {}
@@ -244,26 +237,30 @@ def tile_tpmslimbrouter_pa_t_kernel(
         gate = {}
         update = {}
 
-        def project(g):
+        def start_projected(g):
             projected[g] = ring.tile([P, GROUP_TILES, FEATURES], F32, name="projected")
-            for a in range(GROUP_TILES):
-                tokens = slice(a * P, (a + 1) * P)
-                bank = banks.tile([P, FEATURES], F32, tag="bank")
-                nc.tensor.matmul_mx(
-                    out=bank[:],
-                    lhsT=x_codes[g][:, tokens].bitcast(FP8X4),
-                    lhsT_scale=x_scales[g][:, tokens],
-                    rhs=route_codes[:].bitcast(FP8X4),
-                    rhs_scale=route_scales[:],
-                    start=True,
-                    stop=True,
-                )
-                nc.vector.tensor_tensor(
-                    out=projected[g][:, a, :].rearrange("r (u e p) -> r u e p", u=2, e=2),
-                    in0=bank[:].rearrange("r (u e p) -> r u e p", u=2, e=2),
-                    in1=b_route_bf[:].rearrange("r (u p e) -> r u e p", u=2, e=2),
-                    op=ALU.add,
-                )
+
+        def project(g, a):
+            tokens = slice(a * P, (a + 1) * P)
+            bank = banks.tile([P, FEATURES], F32, tag="bank")
+            nc.tensor.matmul_mx(
+                out=bank[:],
+                lhsT=x_codes[g][:, tokens].bitcast(FP8X4),
+                lhsT_scale=x_scales[g][:, tokens],
+                rhs=route_codes[:].bitcast(FP8X4),
+                rhs_scale=route_scales[:],
+                start=True,
+                stop=True,
+            )
+            return bank
+
+        def add_route_bias(g, a, bank):
+            nc.vector.tensor_tensor(
+                out=projected[g][:, a, :].rearrange("r (u e p) -> r u e p", u=2, e=2),
+                in0=bank[:].rearrange("r (u e p) -> r u e p", u=2, e=2),
+                in1=b_route_bf[:].rearrange("r (u p e) -> r u e p", u=2, e=2),
+                op=ALU.add,
+            )
 
         def start_routed(g):
             routed_grouped[g] = ring.tile([P, GROUP, PACK], BF16, name="routed_grouped", align_bytes=64)
@@ -271,9 +268,15 @@ def tile_tpmslimbrouter_pa_t_kernel(
             routed_scales[g] = ring.tile([P, GROUP], U8, name="routed_scales", align_bytes=64)
             difference[g] = ring.tile([P, CHUNKS, GROUP], F32, name="difference")
 
-        def mix_limbs(g, a):
+        def projects_next(g, a):
+            return g + 1 < GROUPS and a < GROUP_TILES - 1
+
+        def mix_limbs(g, a, jobs=(), early=1):
             tokens = slice(a * P, (a + 1) * P)
-            bank = banks.tile([P, CHUNKS, P], F32, tag="bank")
+            bank = banks.tile([P, CHUNKS, P], F32, name="routed_bank", tag="bank")
+            transposes = [(job, k) for job in jobs for k in range(4)]
+            gaps = [0, 2, 3] if early else [2, 3]
+            share = -(-len(transposes) // len(gaps))
             for c in range(CHUNKS):
                 nc.tensor.matmul(
                     out=bank[:, c, :],
@@ -282,7 +285,16 @@ def tile_tpmslimbrouter_pa_t_kernel(
                     start=True,
                     stop=True,
                 )
-            nc.scalar.copy(out=routed_grouped[g][:, tokens, :], in_=bank[:].rearrange("p c r -> p r c"))
+                if c == CHUNKS - 1:
+                    nc.scalar.copy(out=routed_grouped[g][:, tokens, :], in_=bank[:].rearrange("p c r -> p r c"))
+                if c == 1 and projects_next(g, a):
+                    next_bank = project(g + 1, a)
+                if c == 2 and projects_next(g, a):
+                    add_route_bias(g + 1, a, next_bank)
+                if c in gaps:
+                    for job, k in transposes[:share]:
+                        job(k)
+                    transposes = transposes[share:]
             return bank
 
         def subtract_x(g, a, bank):
@@ -302,30 +314,30 @@ def tile_tpmslimbrouter_pa_t_kernel(
             update[g] = ring.tile([P, CHUNKS, GROUP], F32, name="update")
 
         def open_gate(g, tokens, multiplier):
+            gate_banks = []
+            next_bank = None
+            for side, codes, scales in ((0, x_codes[g], x_scales[g]), (1, routed_codes[g], routed_scales[g])):
+                for c in range(CHUNKS):
+                    features = slice(c * P, (c + 1) * P)
+                    if side == 0:
+                        gate_banks.append(banks.tile([P, GROUP], F32, name="gate_bank", tag="bank"))
+                    nc.tensor.matmul_mx(
+                        out=gate_banks[c][:, tokens],
+                        lhsT=gate_codes[:, side, features].bitcast(FP8X4),
+                        lhsT_scale=gate_scales[:, side, features],
+                        rhs=codes[:, tokens].bitcast(FP8X4),
+                        rhs_scale=scales[:, tokens],
+                        start=side == 0,
+                        stop=side == 1,
+                    )
+                if side == 0 and g + 1 < GROUPS:
+                    next_bank = project(g + 1, GROUP_TILES - 1)
+            if next_bank is not None:
+                add_route_bias(g + 1, GROUP_TILES - 1, next_bank)
             for c in range(CHUNKS):
-                features = slice(c * P, (c + 1) * P)
-                bank = banks.tile([P, GROUP], F32, tag="bank")
-                nc.tensor.matmul_mx(
-                    out=bank[:, tokens],
-                    lhsT=gate_codes[:, 0, features].bitcast(FP8X4),
-                    lhsT_scale=gate_scales[:, 0, features],
-                    rhs=x_codes[g][:, tokens].bitcast(FP8X4),
-                    rhs_scale=x_scales[g][:, tokens],
-                    start=True,
-                    stop=False,
-                )
-                nc.tensor.matmul_mx(
-                    out=bank[:, tokens],
-                    lhsT=gate_codes[:, 1, features].bitcast(FP8X4),
-                    lhsT_scale=gate_scales[:, 1, features],
-                    rhs=routed_codes[g][:, tokens].bitcast(FP8X4),
-                    rhs_scale=routed_scales[g][:, tokens],
-                    start=False,
-                    stop=True,
-                )
                 nc.scalar.activation(
                     out=gate[g][:, c, tokens],
-                    in_=bank[:, tokens],
+                    in_=gate_banks[c][:, tokens],
                     func=ACT.Sigmoid,
                     bias=b_gate_bf[:, c : c + 1],
                     scale=1.0,
@@ -337,47 +349,60 @@ def tile_tpmslimbrouter_pa_t_kernel(
                     op=ALU.mult,
                 )
 
-        def blend(g, a):
-            tokens = slice(a * P, (a + 1) * P)
+        def transpose_back(g, a):
+            bank = banks.tile([P, CHUNKS, P], F32, name="back_bank", tag="bank")
             n = g * GROUP_TILES + a
-            bank = banks.tile([P, CHUNKS, P], F32, tag="bank")
-            for c in range(CHUNKS):
-                nc.tensor.transpose(bank[:, c, :], update[g][:, c, tokens], identity[:])
-            result = ring.tile([P, FEATURES], F32, bufs=4)
-            nc.vector.tensor_tensor(
-                out=result[:].rearrange("r (u p e) -> r u p e", u=2, e=2),
-                in0=bank[:].rearrange("r (u e) p -> r u p e", u=2),
-                in1=x_rows[:, n, :].rearrange("r (u p e) -> r u p e", u=2, e=2),
-                op=ALU.add,
-            )
-            nc.sync.dma_start(out=out_dram[:, n, :], in_=result[:])
 
-        def mix_and_blend(s):
+            def transpose(c):
+                nc.tensor.transpose(bank[:, c, :], update[g][:, c, a * P : (a + 1) * P], identity[:])
+                if c == CHUNKS - 1:
+                    result = ring.tile([P, FEATURES], F32, bufs=4)
+                    nc.vector.tensor_tensor(
+                        out=result[:].rearrange("r (u p e) -> r u p e", u=2, e=2),
+                        in0=bank[:].rearrange("r (u e) p -> r u p e", u=2),
+                        in1=x_rows[:, n, :].rearrange("r (u p e) -> r u p e", u=2, e=2),
+                        op=ALU.add,
+                    )
+                    nc.sync.dma_start(out=out_dram[:, n, :], in_=result[:])
+
+            return transpose
+
+        first_half, second_half = slice(0, GROUP // 2), slice(GROUP // 2, GROUP)
+
+        def step(s):
             start_routed(s)
+            start_projected(s + 1)
+            more_x = s + 2 < GROUPS
+            if more_x:
+                start_x(s + 2)
             for a in range(GROUP_TILES):
-                routed_bank = mix_limbs(s, a)
-                if a == GROUP_TILES - 1:
-                    quantise_routed(s, slice(0, GROUP))
-                if s >= 2:
-                    blend(s - 2, a)
+                jobs = []
+                if more_x and a in (1, 2):
+                    jobs.append(transpose_x(s + 2, a - 1))
+                if s >= 2 and a < 3:
+                    jobs.append(transpose_back(s - 2, a))
+                routed_bank = mix_limbs(s, a, jobs)
+                if a == 3:
+                    quantise_routed(s, second_half)
                 subtract_x(s, a, routed_bank)
-
-        def look_ahead(s):
-            if s + 2 < GROUPS:
-                transpose_x(s + 2)
-                quantise_x(s + 2)
-            if s + 1 < GROUPS:
-                project(s + 1)
+                if a == 1:
+                    quantise_routed(s, first_half)
+            if s >= 2:
+                run(transpose_back(s - 2, 3))
+            start_gate(s)
+            open_gate(s, slice(0, GROUP), nc.gpsimd)
+            if more_x:
+                quantise_x(s + 2, 0)
+                quantise_x(s + 2, 1)
 
         gate_grouped = keep.tile([P, 2, FEATURES, PACK], BF16, align_bytes=64)
         gate_codes = keep.tile([P, 2, FEATURES], U32, align_bytes=64)
         gate_scales = keep.tile([P, 2, FEATURES], U8, align_bytes=64)
         gate_words = gate_rows[:].bitcast(F32)
 
-        def transpose_gate(side):
-            words = gate_words[:, :, side * 2 * P : (side + 1) * 2 * P]
-            for half in range(2):
-                transpose_bank(words[:, 2 * half : 2 * half + 2, :], gate_grouped[:, side, bank_columns(half), :])
+        def transpose_gate(side, half):
+            words = gate_words[:, 2 * half : 2 * half + 2, side * 2 * P : (side + 1) * 2 * P]
+            return transpose_rows(words, gate_grouped[:, side, bank_columns(half), :])
 
         def quantise_gate(side):
             for half in range(2):
@@ -386,58 +411,81 @@ def tile_tpmslimbrouter_pa_t_kernel(
                     gate_grouped[:, side, columns, :], gate_codes[:, side, columns], gate_scales[:, side, columns]
                 )
 
-        project(0)
-        transpose_x(1)
-        quantise_x(1)
+        start_projected(0)
+        first_banks = [project(0, a) for a in range(GROUP_TILES)]
+        add_route_bias(0, 0, first_banks[0])
+        sums_bank = banks.tile([P, FEATURES], F32, tag="bank")
+        nc.tensor.matmul(
+            out=sums_bank[:, 0:LIMBS],
+            lhsT=same_block[:].rearrange("q b j -> q (b j)"),
+            rhs=tanh[:],
+            start=True,
+            stop=True,
+        )
+        row_sum = keep.tile([P, LIMBS], F32)
+        inverse = keep.tile([P, LIMBS], F32)
+        weights = keep.tile([P, LIMBS], F32)
+        nc.vector.tensor_scalar_add(out=row_sum[:], in0=sums_bank[:, 0:LIMBS], scalar1=LIMBS + 2e-6)
+        nc.vector.reciprocal(out=inverse[:], in_=row_sum[:])
+        nc.vector.scalar_tensor_tensor(
+            out=weights[:], in0=tanh[:], scalar=1.0, in1=inverse[:], op0=ALU.add, op1=ALU.mult
+        )
+        nc.vector.tensor_tensor(
+            out=mixer[:],
+            in0=same_position[:].unsqueeze(2).to_broadcast(block_shape),
+            in1=weights[:].unsqueeze(1).to_broadcast(block_shape),
+            op=ALU.mult,
+        )
+        add_route_bias(0, 1, first_banks[1])
+        quantise_x(1, 0)
+        add_route_bias(0, 2, first_banks[2])
+        add_route_bias(0, 3, first_banks[3])
+        quantise_x(1, 1)
         start_routed(0)
-        between = [
-            (lambda: transpose_gate(0), lambda: quantise_gate(0)),
-            (lambda: transpose_gate(1), lambda: quantise_gate(1)),
-            (lambda: transpose_x(2), lambda: quantise_x(2)),
-        ]
+        start_projected(1)
+        start_x(2)
         for a in range(GROUP_TILES):
-            routed_bank = mix_limbs(0, a)
-            if a < len(between):
-                between[a][0]()
-                subtract_x(0, a, routed_bank)
-                between[a][1]()
+            if a < 2:
+                jobs = [transpose_gate(a, 0), transpose_gate(a, 1)]
+            elif a == 2:
+                jobs = [transpose_x(2, 0), transpose_x(2, 1)]
             else:
-                quantise_routed(0, slice(0, GROUP))
-                subtract_x(0, a, routed_bank)
-        project(1)
+                jobs = []
+            routed_bank = mix_limbs(0, a, jobs)
+            if a < 2:
+                quantise_gate(a)
+            if a == 2:
+                quantise_routed(0, first_half)
+                quantise_x(2, 0)
+                quantise_x(2, 1)
+            if a == 3:
+                quantise_routed(0, second_half)
+            subtract_x(0, a, routed_bank)
+        start_gate(0)
+        open_gate(0, slice(0, GROUP), nc.gpsimd)
 
         for s in range(1, GROUPS - 1):
-            start_gate(s - 1)
-            open_gate(s - 1, slice(0, GROUP), nc.gpsimd)
-            mix_and_blend(s)
-            look_ahead(s)
+            step(s)
 
         last = GROUPS - 1
-        first_half, second_half = slice(0, GROUP // 2), slice(GROUP // 2, GROUP)
-        start_gate(last - 1)
-        open_gate(last - 1, slice(0, GROUP), nc.gpsimd)
         start_routed(last)
-        start_gate(last)
         ways_back = [
             [(last - 2, 0), (last - 2, 1)],
             [(last - 2, 2), (last - 2, 3)],
             [(last - 1, 0), (last - 1, 1)],
-            [],
+            [(last - 1, 2), (last - 1, 3)],
         ]
         for a in range(GROUP_TILES):
-            routed_bank = mix_limbs(last, a)
+            routed_bank = mix_limbs(last, a, [transpose_back(*back) for back in ways_back[a]], early=a != 2)
             if a == 1:
                 quantise_routed(last, first_half)
             if a == 3:
                 quantise_routed(last, second_half)
-            for back in ways_back[a][:1]:
-                blend(*back)
             subtract_x(last, a, routed_bank)
-            for back in ways_back[a][1:]:
-                blend(*back)
-        open_gate(last, first_half, nc.gpsimd)
-        blend(last - 1, 2)
-        blend(last - 1, 3)
+            if a == 2:
+                start_gate(last)
+                open_gate(last, first_half, nc.gpsimd)
+        run(transpose_back(last, 0))
         open_gate(last, second_half, nc.vector)
-        for a in range(GROUP_TILES):
-            blend(last, a)
+        for a in range(1, GROUP_TILES):
+            run(transpose_back(last, a))

@@ -268,14 +268,13 @@ def tile_tpmslimbrouter_pa_t_kernel(
             routed_scales[g] = ring.tile([P, GROUP], U8, name="routed_scales", align_bytes=64)
             difference[g] = ring.tile([P, CHUNKS, GROUP], F32, name="difference")
 
-        def projects_next(g, a):
-            return g + 1 < GROUPS and a < GROUP_TILES - 1
+        def new_routed_bank():
+            return banks.tile([P, CHUNKS, P], F32, name="routed_bank", tag="bank")
 
-        def mix_limbs(g, a, jobs=(), early=1):
+        def mix_limbs(g, a, bank, jobs=(), early=True):
             tokens = slice(a * P, (a + 1) * P)
-            bank = banks.tile([P, CHUNKS, P], F32, name="routed_bank", tag="bank")
             transposes = [(job, k) for job in jobs for k in range(4)]
-            gaps = [0, 2, 3] if early else [2, 3]
+            gaps = range(CHUNKS) if early else range(CHUNKS // 2, CHUNKS)
             share = -(-len(transposes) // len(gaps))
             for c in range(CHUNKS):
                 nc.tensor.matmul(
@@ -287,15 +286,10 @@ def tile_tpmslimbrouter_pa_t_kernel(
                 )
                 if c == CHUNKS - 1:
                     nc.scalar.copy(out=routed_grouped[g][:, tokens, :], in_=bank[:].rearrange("p c r -> p r c"))
-                if c == 1 and projects_next(g, a):
-                    next_bank = project(g + 1, a)
-                if c == 2 and projects_next(g, a):
-                    add_route_bias(g + 1, a, next_bank)
                 if c in gaps:
                     for job, k in transposes[:share]:
                         job(k)
                     transposes = transposes[share:]
-            return bank
 
         def subtract_x(g, a, bank):
             tokens = slice(a * P, (a + 1) * P)
@@ -314,26 +308,23 @@ def tile_tpmslimbrouter_pa_t_kernel(
             update[g] = ring.tile([P, CHUNKS, GROUP], F32, name="update")
 
         def open_gate(g, tokens, multiplier):
-            gate_banks = []
-            next_bank = None
-            for side, codes, scales in ((0, x_codes[g], x_scales[g]), (1, routed_codes[g], routed_scales[g])):
-                for c in range(CHUNKS):
-                    features = slice(c * P, (c + 1) * P)
-                    if side == 0:
-                        gate_banks.append(banks.tile([P, GROUP], F32, name="gate_bank", tag="bank"))
-                    nc.tensor.matmul_mx(
-                        out=gate_banks[c][:, tokens],
-                        lhsT=gate_codes[:, side, features].bitcast(FP8X4),
-                        lhsT_scale=gate_scales[:, side, features],
-                        rhs=codes[:, tokens].bitcast(FP8X4),
-                        rhs_scale=scales[:, tokens],
-                        start=side == 0,
-                        stop=side == 1,
-                    )
-                if side == 0 and g + 1 < GROUPS:
-                    next_bank = project(g + 1, GROUP_TILES - 1)
-            if next_bank is not None:
-                add_route_bias(g + 1, GROUP_TILES - 1, next_bank)
+            gate_banks = [None] * CHUNKS
+            sides = ((x_codes[g], x_scales[g]), (routed_codes[g], routed_scales[g]))
+            for first in range(0, CHUNKS, 2):
+                for side, (codes, scales) in enumerate(sides):
+                    for c in (first, first + 1):
+                        features = slice(c * P, (c + 1) * P)
+                        if side == 0:
+                            gate_banks[c] = banks.tile([P, GROUP], F32, name="gate_bank", tag="bank")
+                        nc.tensor.matmul_mx(
+                            out=gate_banks[c][:, tokens],
+                            lhsT=gate_codes[:, side, features].bitcast(FP8X4),
+                            lhsT_scale=gate_scales[:, side, features],
+                            rhs=codes[:, tokens].bitcast(FP8X4),
+                            rhs_scale=scales[:, tokens],
+                            start=side == 0,
+                            stop=side == 1,
+                        )
             for c in range(CHUNKS):
                 nc.scalar.activation(
                     out=gate[g][:, c, tokens],
@@ -371,29 +362,34 @@ def tile_tpmslimbrouter_pa_t_kernel(
 
         def step(s):
             start_routed(s)
-            start_projected(s + 1)
             more_x = s + 2 < GROUPS
             if more_x:
                 start_x(s + 2)
             for a in range(GROUP_TILES):
+                routed_bank = new_routed_bank()
                 jobs = []
                 if more_x and a in (1, 2):
                     jobs.append(transpose_x(s + 2, a - 1))
                 if s >= 2 and a < 3:
                     jobs.append(transpose_back(s - 2, a))
-                routed_bank = mix_limbs(s, a, jobs)
+                mix_limbs(s, a, routed_bank, jobs)
                 if a == 3:
-                    quantise_routed(s, second_half)
+                    if more_x:
+                        quantise_x(s + 2, 0)
+                        quantise_x(s + 2, 1)
+                    quantise_routed(s, slice(0, GROUP))
                 subtract_x(s, a, routed_bank)
-                if a == 1:
-                    quantise_routed(s, first_half)
             if s >= 2:
                 run(transpose_back(s - 2, 3))
+            project_all(s + 1)
             start_gate(s)
             open_gate(s, slice(0, GROUP), nc.gpsimd)
-            if more_x:
-                quantise_x(s + 2, 0)
-                quantise_x(s + 2, 1)
+
+        def project_all(g):
+            start_projected(g)
+            next_banks = [project(g, a) for a in range(GROUP_TILES)]
+            for a in range(GROUP_TILES):
+                add_route_bias(g, a, next_banks[a])
 
         gate_grouped = keep.tile([P, 2, FEATURES, PACK], BF16, align_bytes=64)
         gate_codes = keep.tile([P, 2, FEATURES], U32, align_bytes=64)
@@ -442,25 +438,25 @@ def tile_tpmslimbrouter_pa_t_kernel(
         add_route_bias(0, 3, first_banks[3])
         quantise_x(1, 1)
         start_routed(0)
-        start_projected(1)
         start_x(2)
         for a in range(GROUP_TILES):
+            routed_bank = new_routed_bank()
             if a < 2:
                 jobs = [transpose_gate(a, 0), transpose_gate(a, 1)]
             elif a == 2:
                 jobs = [transpose_x(2, 0), transpose_x(2, 1)]
             else:
                 jobs = []
-            routed_bank = mix_limbs(0, a, jobs)
+            mix_limbs(0, a, routed_bank, jobs)
             if a < 2:
                 quantise_gate(a)
             if a == 2:
-                quantise_routed(0, first_half)
                 quantise_x(2, 0)
                 quantise_x(2, 1)
             if a == 3:
-                quantise_routed(0, second_half)
+                quantise_routed(0, slice(0, GROUP))
             subtract_x(0, a, routed_bank)
+        project_all(1)
         start_gate(0)
         open_gate(0, slice(0, GROUP), nc.gpsimd)
 
@@ -476,7 +472,8 @@ def tile_tpmslimbrouter_pa_t_kernel(
             [(last - 1, 2), (last - 1, 3)],
         ]
         for a in range(GROUP_TILES):
-            routed_bank = mix_limbs(last, a, [transpose_back(*back) for back in ways_back[a]], early=a != 2)
+            routed_bank = new_routed_bank()
+            mix_limbs(last, a, routed_bank, [transpose_back(*back) for back in ways_back[a]], early=a != 2)
             if a == 1:
                 quantise_routed(last, first_half)
             if a == 3:

@@ -26,6 +26,7 @@ GROUP_TILES = 4
 GROUP = GROUP_TILES * P
 GROUPS = TILES // GROUP_TILES
 PSUM_BANKS = 8
+WARM_UPS = 4
 BANK_COLUMNS = 2 * P
 
 FLOPS = 2 * ROWS * FEATURES * FEATURES + 2 * ROWS * 2 * FEATURES * FEATURES + 2 * ROWS * LIMBS * FEATURES
@@ -62,10 +63,11 @@ def tile_tpmslimbrouter_pa_t_kernel(
             for first in range(g * GROUP_TILES, (g + 1) * GROUP_TILES, 2):
                 nc.sync.dma_start(out=x_rows[:, first : first + 2, :], in_=x_dram[:, first : first + 2, :])
 
-        nc.sync.dma_start(
-            out=route_rows[:].rearrange("p (u e) k -> p u (e k)", u=2),
-            in_=W_route.rearrange("(u p e) k -> p u (e k)", u=2, p=P),
-        )
+        for u in range(2):
+            nc.sync.dma_start(
+                out=route_rows[:, 2 * u : 2 * u + 2, :].rearrange("p e k -> p (e k)"),
+                in_=W_route[2 * P * u : 2 * P * (u + 1), :].rearrange("(p e) k -> p (e k)", e=2),
+            )
         load_x(0)
         nc.sync.dma_start(out=b_route_bf[:], in_=b_route.partition_broadcast(P))
         load_x(1)
@@ -186,9 +188,9 @@ def tile_tpmslimbrouter_pa_t_kernel(
             quantise(route_grouped[:, columns, :], route_codes[:, columns], route_scales[:, columns])
 
         def start_x(g):
-            x_grouped[g] = ring.tile([P, GROUP, PACK], BF16, name="x_grouped", bufs=3, align_bytes=64)
-            x_codes[g] = ring.tile([P, GROUP], U32, name="x_codes", bufs=3, align_bytes=64)
-            x_scales[g] = ring.tile([P, GROUP], U8, name="x_scales", bufs=3, align_bytes=64)
+            x_grouped[g] = ring.tile([P, GROUP, PACK], BF16, name="x_grouped", align_bytes=64)
+            x_codes[g] = ring.tile([P, GROUP], U32, name="x_codes", align_bytes=64)
+            x_scales[g] = ring.tile([P, GROUP], U8, name="x_scales", align_bytes=64)
 
         def transpose_x(g, half):
             first = g * GROUP_TILES + 2 * half
@@ -200,8 +202,19 @@ def tile_tpmslimbrouter_pa_t_kernel(
 
         start_x(0)
         start_x(1)
+        warm_bank = banks.tile([P, PACK, P], F32, name="warm_bank", tag="bank")
+
+        def warm_up(times):
+            for k in range(times):
+                nc.tensor.matmul(
+                    out=warm_bank[:, k % PACK, :], lhsT=identity[:], rhs=identity[:], start=True, stop=True
+                )
+
+        warm_up(WARM_UPS)
         run(transpose_route(0))
+        warm_up(1)
         run(transpose_route(1))
+        warm_up(1)
         quantise_route(0)
         waves = keep.tile([P, 2, 3, LIMBS], F32)
         nc.scalar.activation(
@@ -216,16 +229,15 @@ def tile_tpmslimbrouter_pa_t_kernel(
         nc.vector.tensor_reduce(
             out=gyroid[:], in_=products[:].rearrange("p c i -> p i c"), axis=AXIS_X, op=ALU.add
         )
-        quantise_route(1)
         run(transpose_x(0, 0))
-        run(transpose_x(0, 1))
+        warm_up(1)
+        quantise_route(1)
         tanh = keep.tile([P, LIMBS], F32)
         nc.scalar.activation(out=tanh[:], in_=gyroid[:], func=ACT.Tanh, bias=minus_threshold[:, 0:1], scale=1.0)
+        run(transpose_x(0, 1))
         quantise_x(0, 0)
         nc.vector.tensor_tensor(out=tanh[:], in0=tanh[:], in1=own_sign[:], op=ALU.max)
         quantise_x(0, 1)
-        run(transpose_x(1, 0))
-        run(transpose_x(1, 1))
 
         mixer = keep.tile(block_shape, F32)
         mixer_flat = mixer[:].rearrange("q b i -> q (b i)")
@@ -310,9 +322,9 @@ def tile_tpmslimbrouter_pa_t_kernel(
         def open_gate(g, tokens, multiplier):
             gate_banks = [None] * CHUNKS
             sides = ((x_codes[g], x_scales[g]), (routed_codes[g], routed_scales[g]))
-            for first in range(0, CHUNKS, 2):
+            for chunks in ((0, 1, 2), (3,)):
                 for side, (codes, scales) in enumerate(sides):
-                    for c in (first, first + 1):
+                    for c in chunks:
                         features = slice(c * P, (c + 1) * P)
                         if side == 0:
                             gate_banks[c] = banks.tile([P, GROUP], F32, name="gate_bank", tag="bank")
@@ -362,34 +374,32 @@ def tile_tpmslimbrouter_pa_t_kernel(
 
         def step(s):
             start_routed(s)
-            more_x = s + 2 < GROUPS
-            if more_x:
-                start_x(s + 2)
+            start_x(s + 1)
             for a in range(GROUP_TILES):
-                routed_bank = new_routed_bank()
                 jobs = []
-                if more_x and a in (1, 2):
-                    jobs.append(transpose_x(s + 2, a - 1))
+                if s >= 2 and a == 3:
+                    jobs.append(transpose_back(s - 2, a))
+                routed_bank = new_routed_bank()
+                if a < 2:
+                    jobs.append(transpose_x(s + 1, a))
                 if s >= 2 and a < 3:
                     jobs.append(transpose_back(s - 2, a))
                 mix_limbs(s, a, routed_bank, jobs)
+                if a == 2:
+                    quantise_x(s + 1, 0)
+                    quantise_x(s + 1, 1)
                 if a == 3:
-                    if more_x:
-                        quantise_x(s + 2, 0)
-                        quantise_x(s + 2, 1)
                     quantise_routed(s, slice(0, GROUP))
                 subtract_x(s, a, routed_bank)
-            if s >= 2:
-                run(transpose_back(s - 2, 3))
             project_all(s + 1)
             start_gate(s)
             open_gate(s, slice(0, GROUP), nc.gpsimd)
 
         def project_all(g):
             start_projected(g)
-            next_banks = [project(g, a) for a in range(GROUP_TILES)]
+            projected_banks = [project(g, a) for a in range(GROUP_TILES)]
             for a in range(GROUP_TILES):
-                add_route_bias(g, a, next_banks[a])
+                add_route_bias(g, a, projected_banks[a])
 
         gate_grouped = keep.tile([P, 2, FEATURES, PACK], BF16, align_bytes=64)
         gate_codes = keep.tile([P, 2, FEATURES], U32, align_bytes=64)
@@ -408,8 +418,7 @@ def tile_tpmslimbrouter_pa_t_kernel(
                 )
 
         start_projected(0)
-        first_banks = [project(0, a) for a in range(GROUP_TILES)]
-        add_route_bias(0, 0, first_banks[0])
+        first_banks = [project(0, 0), project(0, 1)]
         sums_bank = banks.tile([P, FEATURES], F32, tag="bank")
         nc.tensor.matmul(
             out=sums_bank[:, 0:LIMBS],
@@ -418,6 +427,9 @@ def tile_tpmslimbrouter_pa_t_kernel(
             start=True,
             stop=True,
         )
+        first_banks += [project(0, 2), project(0, 3)]
+        add_route_bias(0, 0, first_banks[0])
+        run(transpose_x(1, 0))
         row_sum = keep.tile([P, LIMBS], F32)
         inverse = keep.tile([P, LIMBS], F32)
         weights = keep.tile([P, LIMBS], F32)
@@ -436,24 +448,21 @@ def tile_tpmslimbrouter_pa_t_kernel(
         quantise_x(1, 0)
         add_route_bias(0, 2, first_banks[2])
         add_route_bias(0, 3, first_banks[3])
-        quantise_x(1, 1)
         start_routed(0)
-        start_x(2)
         for a in range(GROUP_TILES):
             routed_bank = new_routed_bank()
-            if a < 2:
-                jobs = [transpose_gate(a, 0), transpose_gate(a, 1)]
-            elif a == 2:
-                jobs = [transpose_x(2, 0), transpose_x(2, 1)]
-            else:
+            if a == 0:
+                jobs = [transpose_x(1, 1)]
+            elif a == 3:
                 jobs = []
+            else:
+                jobs = [transpose_gate(a - 1, 0), transpose_gate(a - 1, 1)]
             mix_limbs(0, a, routed_bank, jobs)
-            if a < 2:
-                quantise_gate(a)
-            if a == 2:
-                quantise_x(2, 0)
-                quantise_x(2, 1)
-            if a == 3:
+            if a == 0:
+                quantise_x(1, 1)
+            elif a < 3:
+                quantise_gate(a - 1)
+            else:
                 quantise_routed(0, slice(0, GROUP))
             subtract_x(0, a, routed_bank)
         project_all(1)

@@ -188,17 +188,16 @@ def tile_tpmslimbrouter_pa_t_kernel(
             quantise(route_grouped[:, columns, :], route_codes[:, columns], route_scales[:, columns])
 
         def start_x(g):
-            x_grouped[g] = ring.tile([P, GROUP, PACK], BF16, name="x_grouped", align_bytes=64)
-            x_codes[g] = ring.tile([P, GROUP], U32, name="x_codes", align_bytes=64)
-            x_scales[g] = ring.tile([P, GROUP], U8, name="x_scales", align_bytes=64)
+            x_grouped[g] = ring.tile([P, GROUP, PACK], BF16, name="x_grouped", bufs=3, align_bytes=64)
+            x_codes[g] = ring.tile([P, GROUP], U32, name="x_codes", bufs=3, align_bytes=64)
+            x_scales[g] = ring.tile([P, GROUP], U8, name="x_scales", bufs=3, align_bytes=64)
 
         def transpose_x(g, half):
             first = g * GROUP_TILES + 2 * half
             return transpose_rows(x_words[:, first : first + 2, :], x_grouped[g][:, bank_columns(half), :])
 
-        def quantise_x(g, half):
-            columns = bank_columns(half)
-            quantise(x_grouped[g][:, columns, :], x_codes[g][:, columns], x_scales[g][:, columns])
+        def quantise_x(g, tokens):
+            quantise(x_grouped[g][:, tokens, :], x_codes[g][:, tokens], x_scales[g][:, tokens])
 
         start_x(0)
         start_x(1)
@@ -235,9 +234,9 @@ def tile_tpmslimbrouter_pa_t_kernel(
         tanh = keep.tile([P, LIMBS], F32)
         nc.scalar.activation(out=tanh[:], in_=gyroid[:], func=ACT.Tanh, bias=minus_threshold[:, 0:1], scale=1.0)
         run(transpose_x(0, 1))
-        quantise_x(0, 0)
+        quantise_x(0, bank_columns(0))
         nc.vector.tensor_tensor(out=tanh[:], in0=tanh[:], in1=own_sign[:], op=ALU.max)
-        quantise_x(0, 1)
+        quantise_x(0, bank_columns(1))
 
         mixer = keep.tile(block_shape, F32)
         mixer_flat = mixer[:].rearrange("q b i -> q (b i)")
@@ -319,7 +318,7 @@ def tile_tpmslimbrouter_pa_t_kernel(
             gate[g] = ring.tile([P, CHUNKS, GROUP], F32, name="gate")
             update[g] = ring.tile([P, CHUNKS, GROUP], F32, name="update")
 
-        def open_gate(g, tokens, multiplier):
+        def open_gate(g, tokens, multipliers):
             gate_banks = [None] * CHUNKS
             sides = ((x_codes[g], x_scales[g]), (routed_codes[g], routed_scales[g]))
             for chunks in ((0, 1, 2), (3,)):
@@ -345,7 +344,7 @@ def tile_tpmslimbrouter_pa_t_kernel(
                     bias=b_gate_bf[:, c : c + 1],
                     scale=1.0,
                 )
-                multiplier.tensor_tensor(
+                multipliers[c].tensor_tensor(
                     out=update[g][:, c, tokens],
                     in0=gate[g][:, c, tokens],
                     in1=difference[g][:, c, tokens],
@@ -374,26 +373,38 @@ def tile_tpmslimbrouter_pa_t_kernel(
 
         def step(s):
             start_routed(s)
-            start_x(s + 1)
+            more_x = s + 2 < GROUPS
+            if s == 1:
+                start_x(2)
+            if more_x:
+                start_x(s + 2)
             for a in range(GROUP_TILES):
                 jobs = []
                 if s >= 2 and a == 3:
                     jobs.append(transpose_back(s - 2, a))
                 routed_bank = new_routed_bank()
-                if a < 2:
-                    jobs.append(transpose_x(s + 1, a))
                 if s >= 2 and a < 3:
                     jobs.append(transpose_back(s - 2, a))
-                mix_limbs(s, a, routed_bank, jobs)
-                if a == 2:
-                    quantise_x(s + 1, 0)
-                    quantise_x(s + 1, 1)
+                if s == 1 and a == 0:
+                    jobs += [transpose_x(2, 0), transpose_x(2, 1)]
+                if more_x and a in (1, 2):
+                    jobs.append(transpose_x(s + 2, a - 1))
                 if a == 3:
-                    quantise_routed(s, slice(0, GROUP))
+                    quantise_routed(s, slice(0, 2 * P))
+                    quantise_routed(s, slice(2 * P, 3 * P))
+                    if more_x:
+                        quantise_x(s + 2, bank_columns(0))
+                mix_limbs(s, a, routed_bank, jobs)
+                if s == 1 and a == 2:
+                    quantise_x(2, slice(0, GROUP))
+                if a == 3:
+                    quantise_routed(s, slice(3 * P, GROUP))
+                    if more_x:
+                        quantise_x(s + 2, bank_columns(1))
                 subtract_x(s, a, routed_bank)
             project_all(s + 1)
             start_gate(s)
-            open_gate(s, slice(0, GROUP), nc.gpsimd)
+            open_gate(s, slice(0, GROUP), [nc.gpsimd] * CHUNKS)
 
         def project_all(g):
             start_projected(g)
@@ -445,7 +456,7 @@ def tile_tpmslimbrouter_pa_t_kernel(
             op=ALU.mult,
         )
         add_route_bias(0, 1, first_banks[1])
-        quantise_x(1, 0)
+        quantise_x(1, bank_columns(0))
         add_route_bias(0, 2, first_banks[2])
         add_route_bias(0, 3, first_banks[3])
         start_routed(0)
@@ -459,7 +470,7 @@ def tile_tpmslimbrouter_pa_t_kernel(
                 jobs = [transpose_gate(a - 1, 0), transpose_gate(a - 1, 1)]
             mix_limbs(0, a, routed_bank, jobs)
             if a == 0:
-                quantise_x(1, 1)
+                quantise_x(1, bank_columns(1))
             elif a < 3:
                 quantise_gate(a - 1)
             else:
@@ -467,7 +478,7 @@ def tile_tpmslimbrouter_pa_t_kernel(
             subtract_x(0, a, routed_bank)
         project_all(1)
         start_gate(0)
-        open_gate(0, slice(0, GROUP), nc.gpsimd)
+        open_gate(0, slice(0, GROUP), [nc.gpsimd] * CHUNKS)
 
         for s in range(1, GROUPS - 1):
             step(s)
@@ -490,8 +501,8 @@ def tile_tpmslimbrouter_pa_t_kernel(
             subtract_x(last, a, routed_bank)
             if a == 2:
                 start_gate(last)
-                open_gate(last, first_half, nc.gpsimd)
+                open_gate(last, first_half, [nc.vector] * CHUNKS)
         run(transpose_back(last, 0))
-        open_gate(last, second_half, nc.vector)
+        open_gate(last, second_half, [nc.vector] * CHUNKS)
         for a in range(1, GROUP_TILES):
             run(transpose_back(last, a))

@@ -26,7 +26,7 @@ GROUP_TILES = 4
 GROUP = GROUP_TILES * P
 GROUPS = TILES // GROUP_TILES
 PSUM_BANKS = 8
-WARM_UPS = 4
+WARM_UPS = 3
 BANK_COLUMNS = 2 * P
 
 FLOPS = 2 * ROWS * FEATURES * FEATURES + 2 * ROWS * 2 * FEATURES * FEATURES + 2 * ROWS * LIMBS * FEATURES
@@ -282,10 +282,9 @@ def tile_tpmslimbrouter_pa_t_kernel(
         def new_routed_bank():
             return banks.tile([P, CHUNKS, P], F32, name="routed_bank", tag="bank")
 
-        def mix_limbs(g, a, bank, jobs=(), early=True):
+        def mix_limbs(g, a, bank, jobs=(), gaps=range(CHUNKS)):
             tokens = slice(a * P, (a + 1) * P)
             transposes = [(job, k) for job in jobs for k in range(4)]
-            gaps = range(CHUNKS) if early else range(CHUNKS // 2, CHUNKS)
             share = -(-len(transposes) // len(gaps))
             for c in range(CHUNKS):
                 nc.tensor.matmul(
@@ -394,7 +393,9 @@ def tile_tpmslimbrouter_pa_t_kernel(
                     quantise_routed(s, slice(2 * P, 3 * P))
                     if more_x:
                         quantise_x(s + 2, bank_columns(0))
-                mix_limbs(s, a, routed_bank, jobs)
+                first_gap = 1 if a == 0 else 0
+                last_gap = CHUNKS - 2 if a == 3 else CHUNKS - 1
+                mix_limbs(s, a, routed_bank, jobs, range(first_gap, last_gap + 1))
                 if s == 1 and a == 2:
                     quantise_x(2, slice(0, GROUP))
                 if a == 3:
@@ -428,8 +429,6 @@ def tile_tpmslimbrouter_pa_t_kernel(
                     gate_grouped[:, side, columns, :], gate_codes[:, side, columns], gate_scales[:, side, columns]
                 )
 
-        start_projected(0)
-        first_banks = [project(0, 0), project(0, 1)]
         sums_bank = banks.tile([P, FEATURES], F32, tag="bank")
         nc.tensor.matmul(
             out=sums_bank[:, 0:LIMBS],
@@ -438,8 +437,8 @@ def tile_tpmslimbrouter_pa_t_kernel(
             start=True,
             stop=True,
         )
-        first_banks += [project(0, 2), project(0, 3)]
-        add_route_bias(0, 0, first_banks[0])
+        start_projected(0)
+        first_banks = [project(0, a) for a in range(GROUP_TILES)]
         run(transpose_x(1, 0))
         row_sum = keep.tile([P, LIMBS], F32)
         inverse = keep.tile([P, LIMBS], F32)
@@ -449,6 +448,7 @@ def tile_tpmslimbrouter_pa_t_kernel(
         nc.vector.scalar_tensor_tensor(
             out=weights[:], in0=tanh[:], scalar=1.0, in1=inverse[:], op0=ALU.add, op1=ALU.mult
         )
+        add_route_bias(0, 0, first_banks[0])
         nc.vector.tensor_tensor(
             out=mixer[:],
             in0=same_position[:].unsqueeze(2).to_broadcast(block_shape),
@@ -485,24 +485,20 @@ def tile_tpmslimbrouter_pa_t_kernel(
 
         last = GROUPS - 1
         start_routed(last)
-        ways_back = [
-            [(last - 2, 0), (last - 2, 1)],
-            [(last - 2, 2), (last - 2, 3)],
-            [(last - 1, 0), (last - 1, 1)],
-            [(last - 1, 2), (last - 1, 3)],
-        ]
+        ways_back = [[(last - 2, 0), (last - 2, 1)], [(last - 2, 2), (last - 2, 3)], [], [(last - 1, 0), (last - 1, 1)]]
         for a in range(GROUP_TILES):
             routed_bank = new_routed_bank()
-            mix_limbs(last, a, routed_bank, [transpose_back(*back) for back in ways_back[a]], early=a != 2)
-            if a == 1:
+            jobs = [transpose_back(*back) for back in ways_back[a]]
+            mix_limbs(last, a, routed_bank, jobs, [2, 3] if a == 3 else range(CHUNKS))
+            if a == 2:
                 quantise_routed(last, first_half)
             if a == 3:
                 quantise_routed(last, second_half)
             subtract_x(last, a, routed_bank)
-            if a == 2:
-                start_gate(last)
-                open_gate(last, first_half, [nc.vector] * CHUNKS)
-        run(transpose_back(last, 0))
+        start_gate(last)
+        open_gate(last, first_half, [nc.vector] * CHUNKS)
+        run(transpose_back(last - 1, 2))
+        run(transpose_back(last - 1, 3))
         open_gate(last, second_half, [nc.vector] * CHUNKS)
-        for a in range(1, GROUP_TILES):
+        for a in range(GROUP_TILES):
             run(transpose_back(last, a))

@@ -71,10 +71,11 @@ def tile_tpmslimbrouter_pa_t_kernel(
         load_x(0)
         nc.sync.dma_start(out=b_route_bf[:], in_=b_route.partition_broadcast(P))
         load_x(1)
-        nc.sync.dma_start(
-            out=gate_rows[:].rearrange("p (u e) k -> p u (e k)", u=2),
-            in_=W_gate.rearrange("(u p e) k -> p u (e k)", u=2, p=P),
-        )
+        for u in range(2):
+            nc.sync.dma_start(
+                out=gate_rows[:, 2 * u : 2 * u + 2, :].rearrange("p e k -> p (e k)"),
+                in_=W_gate[2 * P * u : 2 * P * (u + 1), :].rearrange("(p e) k -> p (e k)", e=2),
+            )
         load_x(2)
         nc.sync.dma_start(
             out=b_gate_bf[:].rearrange("p (u e) -> p u e", u=2),
@@ -212,13 +213,12 @@ def tile_tpmslimbrouter_pa_t_kernel(
         warm_up(WARM_UPS)
         run(transpose_route(0))
         warm_up(1)
-        run(transpose_route(1))
-        warm_up(1)
-        quantise_route(0)
         waves = keep.tile([P, 2, 3, LIMBS], F32)
         nc.scalar.activation(
             out=waves[:].rearrange("p w c i -> p (w c i)"), in_=folded[:], func=ACT.Sin, scale=2.0 * math.pi
         )
+        run(transpose_route(1))
+        warm_up(1)
         products = keep.tile(plane_shape, F32)
         gyroid = keep.tile([P, LIMBS], F32)
         minus_threshold = keep.tile([P, 1], F32)
@@ -228,14 +228,15 @@ def tile_tpmslimbrouter_pa_t_kernel(
         nc.vector.tensor_reduce(
             out=gyroid[:], in_=products[:].rearrange("p c i -> p i c"), axis=AXIS_X, op=ALU.add
         )
-        run(transpose_x(0, 0))
-        warm_up(1)
-        quantise_route(1)
         tanh = keep.tile([P, LIMBS], F32)
         nc.scalar.activation(out=tanh[:], in_=gyroid[:], func=ACT.Tanh, bias=minus_threshold[:, 0:1], scale=1.0)
+        quantise_route(0)
+        run(transpose_x(0, 0))
+        warm_up(1)
+        nc.vector.tensor_tensor(out=tanh[:], in0=tanh[:], in1=own_sign[:], op=ALU.max)
+        quantise_route(1)
         run(transpose_x(0, 1))
         quantise_x(0, bank_columns(0))
-        nc.vector.tensor_tensor(out=tanh[:], in0=tanh[:], in1=own_sign[:], op=ALU.max)
         quantise_x(0, bank_columns(1))
 
         mixer = keep.tile(block_shape, F32)
@@ -317,7 +318,7 @@ def tile_tpmslimbrouter_pa_t_kernel(
             gate[g] = ring.tile([P, CHUNKS, GROUP], F32, name="gate")
             update[g] = ring.tile([P, CHUNKS, GROUP], F32, name="update")
 
-        def open_gate(g, tokens, multipliers):
+        def open_gate(g, tokens):
             gate_banks = [None] * CHUNKS
             sides = ((x_codes[g], x_scales[g]), (routed_codes[g], routed_scales[g]))
             for chunks in ((0, 1, 2), (3,)):
@@ -343,7 +344,10 @@ def tile_tpmslimbrouter_pa_t_kernel(
                     bias=b_gate_bf[:, c : c + 1],
                     scale=1.0,
                 )
-                multipliers[c].tensor_tensor(
+
+        def multiply(g, tokens, chunks, engine):
+            for c in chunks:
+                engine.tensor_tensor(
                     out=update[g][:, c, tokens],
                     in0=gate[g][:, c, tokens],
                     in1=difference[g][:, c, tokens],
@@ -405,7 +409,8 @@ def tile_tpmslimbrouter_pa_t_kernel(
                 subtract_x(s, a, routed_bank)
             project_all(s + 1)
             start_gate(s)
-            open_gate(s, slice(0, GROUP), [nc.gpsimd] * CHUNKS)
+            open_gate(s, slice(0, GROUP))
+            multiply(s, slice(0, GROUP), range(CHUNKS), nc.gpsimd)
 
         def project_all(g):
             start_projected(g)
@@ -422,12 +427,9 @@ def tile_tpmslimbrouter_pa_t_kernel(
             words = gate_words[:, 2 * half : 2 * half + 2, side * 2 * P : (side + 1) * 2 * P]
             return transpose_rows(words, gate_grouped[:, side, bank_columns(half), :])
 
-        def quantise_gate(side):
-            for half in range(2):
-                columns = bank_columns(half)
-                quantise(
-                    gate_grouped[:, side, columns, :], gate_codes[:, side, columns], gate_scales[:, side, columns]
-                )
+        def quantise_gate(side, half):
+            columns = bank_columns(half)
+            quantise(gate_grouped[:, side, columns, :], gate_codes[:, side, columns], gate_scales[:, side, columns])
 
         sums_bank = banks.tile([P, FEATURES], F32, tag="bank")
         nc.tensor.matmul(
@@ -440,6 +442,7 @@ def tile_tpmslimbrouter_pa_t_kernel(
         start_projected(0)
         first_banks = [project(0, a) for a in range(GROUP_TILES)]
         run(transpose_x(1, 0))
+        run(transpose_x(1, 1))
         row_sum = keep.tile([P, LIMBS], F32)
         inverse = keep.tile([P, LIMBS], F32)
         weights = keep.tile([P, LIMBS], F32)
@@ -456,29 +459,26 @@ def tile_tpmslimbrouter_pa_t_kernel(
             op=ALU.mult,
         )
         add_route_bias(0, 1, first_banks[1])
-        quantise_x(1, bank_columns(0))
         add_route_bias(0, 2, first_banks[2])
         add_route_bias(0, 3, first_banks[3])
+        quantise_x(1, slice(0, GROUP))
         start_routed(0)
         for a in range(GROUP_TILES):
             routed_bank = new_routed_bank()
-            if a == 0:
-                jobs = [transpose_x(1, 1)]
-            elif a == 3:
-                jobs = []
-            else:
-                jobs = [transpose_gate(a - 1, 0), transpose_gate(a - 1, 1)]
+            jobs = [transpose_gate(0, a), transpose_gate(1, a)] if a < 2 else []
             mix_limbs(0, a, routed_bank, jobs)
-            if a == 0:
-                quantise_x(1, bank_columns(1))
-            elif a < 3:
-                quantise_gate(a - 1)
-            else:
+            if a == 3:
                 quantise_routed(0, slice(0, GROUP))
+            if a < 2:
+                quantise_gate(0, a)
             subtract_x(0, a, routed_bank)
+            if a < 2:
+                quantise_gate(1, a)
         project_all(1)
         start_gate(0)
-        open_gate(0, slice(0, GROUP), [nc.gpsimd] * CHUNKS)
+        open_gate(0, slice(0, GROUP))
+        multiply(0, slice(0, GROUP), (0, 1), nc.gpsimd)
+        multiply(0, slice(0, GROUP), (2, 3), nc.vector)
 
         for s in range(1, GROUPS - 1):
             step(s)
@@ -496,9 +496,12 @@ def tile_tpmslimbrouter_pa_t_kernel(
                 quantise_routed(last, second_half)
             subtract_x(last, a, routed_bank)
         start_gate(last)
-        open_gate(last, first_half, [nc.vector] * CHUNKS)
+        open_gate(last, first_half)
+        multiply(last, first_half, (0, 1), nc.gpsimd)
         run(transpose_back(last - 1, 2))
         run(transpose_back(last - 1, 3))
-        open_gate(last, second_half, [nc.vector] * CHUNKS)
+        multiply(last, first_half, (2, 3), nc.vector)
+        open_gate(last, second_half)
+        multiply(last, second_half, range(CHUNKS), nc.vector)
         for a in range(GROUP_TILES):
             run(transpose_back(last, a))

import math
from contextlib import ExitStack

import concourse.masks as masks
import concourse.mybir as mybir

F32 = mybir.dt.float32
BF16 = mybir.dt.bfloat16
I32 = mybir.dt.int32
U32 = mybir.dt.uint32
U8 = mybir.dt.uint8
FP8X4 = mybir.dt.float8_e4m3fn_x4
ALU = mybir.AluOpType
ACT = mybir.ActivationFunctionType
AXIS_X = mybir.AxisListType.X

P = 128
PACK = 4
LIMBS = 8
FEATURES = 512
CHUNKS = FEATURES // P
ROWS = 2 * 256 * LIMBS
TILES = ROWS // P
POSITIONS = P // LIMBS
GROUP_TILES = 4
GROUP = GROUP_TILES * P
GROUPS = TILES // GROUP_TILES
PSUM_BANKS = 8
WARM_UPS = 3
BANK_COLUMNS = 2 * P

FLOPS = 2 * ROWS * FEATURES * FEATURES + 2 * ROWS * 2 * FEATURES * FEATURES + 2 * ROWS * LIMBS * FEATURES


def tile_tpmslimbrouter_pa_t_kernel(
    tc, x, limb_positions, channel_threshold, W_route, b_route, W_gate, b_gate, out
):
    nc = tc.nc
    x_dram = x.rearrange("b s l h -> (b s l) h").rearrange("(n p) h -> p n h", p=P)
    out_dram = out.rearrange("b s l h -> (b s l) h").rearrange("(n p) h -> p n h", p=P)

    with ExitStack() as ctx:
        keep = ctx.enter_context(tc.tile_pool(name="keep", bufs=1))
        ring = ctx.enter_context(tc.tile_pool(name="ring", bufs=2))
        banks = ctx.enter_context(tc.psum_pool(name="banks", bufs=PSUM_BANKS))
        ctx.enter_context(tc.manual_schedule())

        positions_bf = keep.tile([P, LIMBS, 3], BF16)
        threshold_bf = keep.tile([P, 1], BF16)
        b_route_bf = keep.tile([P, FEATURES], BF16)
        b_gate_bf = keep.tile([P, CHUNKS], BF16)
        nc.sync.dma_start(
            out=positions_bf[:].rearrange("p l c -> p (l c)"),
            in_=limb_positions.rearrange("l c -> (l c)").partition_broadcast(P),
        )
        nc.sync.dma_start(out=threshold_bf[:], in_=channel_threshold.partition_broadcast(P))

        route_rows = keep.tile([P, CHUNKS, FEATURES], BF16)
        gate_rows = keep.tile([P, CHUNKS, 2 * FEATURES], BF16)
        x_rows = keep.tile([P, TILES, FEATURES], BF16)

        def load_x(g):
            for first in range(g * GROUP_TILES, (g + 1) * GROUP_TILES, 2):
                nc.sync.dma_start(out=x_rows[:, first : first + 2, :], in_=x_dram[:, first : first + 2, :])

        for u in range(2):
            nc.sync.dma_start(
                out=route_rows[:, 2 * u : 2 * u + 2, :].rearrange("p e k -> p (e k)"),
                in_=W_route[2 * P * u : 2 * P * (u + 1), :].rearrange("(p e) k -> p (e k)", e=2),
            )
        load_x(0)
        nc.sync.dma_start(out=b_route_bf[:], in_=b_route.partition_broadcast(P))
        load_x(1)
        for u in range(2):
            nc.sync.dma_start(
                out=gate_rows[:, 2 * u : 2 * u + 2, :].rearrange("p e k -> p (e k)"),
                in_=W_gate[2 * P * u : 2 * P * (u + 1), :].rearrange("(p e) k -> p (e k)", e=2),
            )
        load_x(2)
        nc.sync.dma_start(
            out=b_gate_bf[:].rearrange("p (u e) -> p u e", u=2),
            in_=b_gate.rearrange("(u p e) -> p u e", u=2, p=P),
        )
        for g in range(3, GROUPS):
            load_x(g)

        identity = keep.tile([P, P], F32)
        masks.make_identity(nc, identity[:])
        table_warmer = keep.tile([P, 1], F32)
        nc.vector.memset(table_warmer[:], 0.0)
        nc.scalar.activation(out=table_warmer[:], in_=table_warmer[:], func=ACT.Silu)

        def transpose_rows(rows_words, grouped):
            bank = banks.tile([P, 2, 2, P], F32, name="rows_bank", tag="bank")

            def transpose(k):
                i, u = divmod(k, 2)
                nc.tensor.transpose(bank[:, i, u, :], rows_words[:, i, u * P : (u + 1) * P], identity[:])
                if k == 3:
                    nc.scalar.copy(
                        out=grouped.bitcast(F32).rearrange("p (i r) u -> p i r u", i=2),
                        in_=bank[:].rearrange("p i u r -> p i r u"),
                    )

            return transpose

        def run(job):
            for k in range(4):
                job(k)

        def quantise(grouped, codes, scales):
            nc.vector.quantize_mx(
                out=codes.bitcast(FP8X4), scales=scales, in_=grouped.rearrange("p r t -> p (r t)")
            )

        def bank_columns(half):
            return slice(half * BANK_COLUMNS, (half + 1) * BANK_COLUMNS)

        own_limb = keep.tile([P, LIMBS], F32)
        own_sign = keep.tile([P, LIMBS], F32)
        same_position = keep.tile([P, POSITIONS], F32)
        same_block = keep.tile([P, POSITIONS, LIMBS], F32)
        block_shape = [P, POSITIONS, LIMBS]
        nc.vector.tensor_reduce(
            out=own_limb[:], in_=identity[:].rearrange("q (b j) -> q j b", j=LIMBS), axis=AXIS_X, op=ALU.add
        )
        nc.vector.tensor_reduce(
            out=same_position[:], in_=identity[:].rearrange("q (b j) -> q b j", j=LIMBS), axis=AXIS_X, op=ALU.add
        )
        nc.vector.tensor_scalar(
            out=own_sign[:], in0=own_limb[:], scalar1=2.0, scalar2=-1.0, op0=ALU.mult, op1=ALU.add
        )
        nc.vector.tensor_copy(out=same_block[:], in_=same_position[:].unsqueeze(2).to_broadcast(block_shape))

        plane_shape = [P, 3, LIMBS]
        positions = positions_bf[:].rearrange("p l c -> p c l")
        per_turn = 1.0 / (4.0 * math.pi)
        own_terms = keep.tile(plane_shape, F32)
        own_turns = keep.tile([P, 3], F32)
        turns = keep.tile([P, 2, 3, LIMBS], F32)
        nc.vector.scalar_tensor_tensor(
            out=own_terms[:],
            in0=positions,
            scalar=per_turn,
            in1=own_limb[:].unsqueeze(1).to_broadcast(plane_shape),
            op0=ALU.mult,
            op1=ALU.mult,
        )
        nc.vector.tensor_reduce(out=own_turns[:], in_=own_terms[:], axis=AXIS_X, op=ALU.add)
        nc.vector.scalar_tensor_tensor(
            out=turns[:, 0],
            in0=positions,
            scalar=per_turn,
            in1=own_turns[:].unsqueeze(2).to_broadcast(plane_shape),
            op0=ALU.mult,
            op1=ALU.add,
        )
        nc.vector.tensor_scalar_add(out=turns[:, 1], in0=turns[:, 0], scalar1=0.25)
        angle_shape = [P, 2 * 3 * LIMBS]
        turns_flat = turns[:].rearrange("p w c i -> p (w c i)")
        whole = keep.tile(angle_shape, I32)
        part = keep.tile(angle_shape, F32)
        flipped = keep.tile(angle_shape, F32)
        folded = keep.tile(angle_shape, F32)
        nc.vector.tensor_copy(out=whole[:], in_=turns_flat)
        nc.vector.tensor_tensor(out=part[:], in0=turns_flat, in1=whole[:], op=ALU.subtract)
        nc.vector.scalar_tensor_tensor(
            out=flipped[:], in0=part[:], scalar=0.5, in1=part[:], op0=ALU.is_gt, op1=ALU.subtract
        )
        nc.vector.scalar_tensor_tensor(
            out=folded[:], in0=flipped[:], scalar=0.5, in1=flipped[:], op0=ALU.is_gt, op1=ALU.subtract
        )
        route_grouped = keep.tile([P, FEATURES, PACK], BF16, align_bytes=64)
        route_codes = keep.tile([P, FEATURES], U32, align_bytes=64)
        route_scales = keep.tile([P, FEATURES], U8, align_bytes=64)
        route_words = route_rows[:].bitcast(F32)
        x_words = x_rows[:].bitcast(F32)
        x_grouped = {}
        x_codes = {}
        x_scales = {}

        def transpose_route(half):
            return transpose_rows(
                route_words[:, 2 * half : 2 * half + 2, :], route_grouped[:, bank_columns(half), :]
            )

        def quantise_route(half):
            columns = bank_columns(half)
            quantise(route_grouped[:, columns, :], route_codes[:, columns], route_scales[:, columns])

        def start_x(g):
            x_grouped[g] = ring.tile([P, GROUP, PACK], BF16, name="x_grouped", bufs=3, align_bytes=64)
            x_codes[g] = ring.tile([P, GROUP], U32, name="x_codes", bufs=3, align_bytes=64)
            x_scales[g] = ring.tile([P, GROUP], U8, name="x_scales", bufs=3, align_bytes=64)

        def transpose_x(g, half):
            first = g * GROUP_TILES + 2 * half
            return transpose_rows(x_words[:, first : first + 2, :], x_grouped[g][:, bank_columns(half), :])

        def quantise_x(g, tokens):
            quantise(x_grouped[g][:, tokens, :], x_codes[g][:, tokens], x_scales[g][:, tokens])

        start_x(0)
        start_x(1)
        warm_bank = banks.tile([P, PACK, P], F32, name="warm_bank", tag="bank")

        def warm_up(times):
            for k in range(times):
                nc.tensor.matmul(
                    out=warm_bank[:, k % PACK, :], lhsT=identity[:], rhs=identity[:], start=True, stop=True
                )

        warm_up(WARM_UPS)
        run(transpose_route(0))
        warm_up(1)
        waves = keep.tile([P, 2, 3, LIMBS], F32)
        nc.scalar.activation(
            out=waves[:].rearrange("p w c i -> p (w c i)"), in_=folded[:], func=ACT.Sin, scale=2.0 * math.pi
        )
        run(transpose_route(1))
        warm_up(1)
        products = keep.tile(plane_shape, F32)
        gyroid = keep.tile([P, LIMBS], F32)
        minus_threshold = keep.tile([P, 1], F32)
        nc.vector.tensor_tensor(out=products[:, 0:2], in0=waves[:, 0, 0:2], in1=waves[:, 1, 1:3], op=ALU.mult)
        nc.vector.tensor_tensor(out=products[:, 2], in0=waves[:, 0, 2], in1=waves[:, 1, 0], op=ALU.mult)
        nc.vector.tensor_scalar_mul(out=minus_threshold[:], in0=threshold_bf[:], scalar1=-1.0)
        nc.vector.tensor_reduce(
            out=gyroid[:], in_=products[:].rearrange("p c i -> p i c"), axis=AXIS_X, op=ALU.add
        )
        tanh = keep.tile([P, LIMBS], F32)
        nc.scalar.activation(out=tanh[:], in_=gyroid[:], func=ACT.Tanh, bias=minus_threshold[:, 0:1], scale=1.0)
        quantise_route(0)
        run(transpose_x(0, 0))
        warm_up(1)
        nc.vector.tensor_tensor(out=tanh[:], in0=tanh[:], in1=own_sign[:], op=ALU.max)
        quantise_route(1)
        run(transpose_x(0, 1))
        quantise_x(0, bank_columns(0))
        quantise_x(0, bank_columns(1))

        mixer = keep.tile(block_shape, F32)
        mixer_flat = mixer[:].rearrange("q b i -> q (b i)")
        projected = {}
        routed_grouped = {}
        routed_codes = {}
        routed_scales = {}
        difference = {}
        gate = {}
        update = {}

        def start_projected(g):
            projected[g] = ring.tile([P, GROUP_TILES, FEATURES], F32, name="projected")

        def project(g, a):
            tokens = slice(a * P, (a + 1) * P)
            bank = banks.tile([P, FEATURES], F32, tag="bank")
            nc.tensor.matmul_mx(
                out=bank[:],
                lhsT=x_codes[g][:, tokens].bitcast(FP8X4),
                lhsT_scale=x_scales[g][:, tokens],
                rhs=route_codes[:].bitcast(FP8X4),
                rhs_scale=route_scales[:],
                start=True,
                stop=True,
            )
            return bank

        def add_route_bias(g, a, bank):
            nc.vector.tensor_tensor(
                out=projected[g][:, a, :].rearrange("r (u e p) -> r u e p", u=2, e=2),
                in0=bank[:].rearrange("r (u e p) -> r u e p", u=2, e=2),
                in1=b_route_bf[:].rearrange("r (u p e) -> r u e p", u=2, e=2),
                op=ALU.add,
            )

        def start_routed(g):
            routed_grouped[g] = ring.tile([P, GROUP, PACK], BF16, name="routed_grouped", align_bytes=64)
            routed_codes[g] = ring.tile([P, GROUP], U32, name="routed_codes", align_bytes=64)
            routed_scales[g] = ring.tile([P, GROUP], U8, name="routed_scales", align_bytes=64)
            difference[g] = ring.tile([P, CHUNKS, GROUP], F32, name="difference")

        def new_routed_bank():
            return banks.tile([P, CHUNKS, P], F32, name="routed_bank", tag="bank")

        def mix_limbs(g, a, bank, jobs=(), gaps=range(CHUNKS)):
            tokens = slice(a * P, (a + 1) * P)
            transposes = [(job, k) for job in jobs for k in range(4)]
            share = -(-len(transposes) // len(gaps))
            for c in range(CHUNKS):
                nc.tensor.matmul(
                    out=bank[:, c, :],
                    lhsT=projected[g][:, a, c * P : (c + 1) * P],
                    rhs=mixer_flat,
                    start=True,
                    stop=True,
                )
                if c == CHUNKS - 1:
                    nc.scalar.copy(out=routed_grouped[g][:, tokens, :], in_=bank[:].rearrange("p c r -> p r c"))
                if c in gaps:
                    for job, k in transposes[:share]:
                        job(k)
                    transposes = transposes[share:]

        def subtract_x(g, a, bank):
            tokens = slice(a * P, (a + 1) * P)
            nc.vector.tensor_tensor(
                out=difference[g][:, :, tokens],
                in0=bank[:],
                in1=x_grouped[g][:, tokens, :].rearrange("p r c -> p c r"),
                op=ALU.subtract,
            )

        def quantise_routed(g, tokens):
            quantise(routed_grouped[g][:, tokens, :], routed_codes[g][:, tokens], routed_scales[g][:, tokens])

        def start_gate(g):
            gate[g] = ring.tile([P, CHUNKS, GROUP], F32, name="gate")
            update[g] = ring.tile([P, CHUNKS, GROUP], F32, name="update")

        def open_gate(g, tokens):
            gate_banks = [None] * CHUNKS
            sides = ((x_codes[g], x_scales[g]), (routed_codes[g], routed_scales[g]))
            for chunks in ((0, 1, 2), (3,)):
                for side, (codes, scales) in enumerate(sides):
                    for c in chunks:
                        features = slice(c * P, (c + 1) * P)
                        if side == 0:
                            gate_banks[c] = banks.tile([P, GROUP], F32, name="gate_bank", tag="bank")
                        nc.tensor.matmul_mx(
                            out=gate_banks[c][:, tokens],
                            lhsT=gate_codes[:, side, features].bitcast(FP8X4),
                            lhsT_scale=gate_scales[:, side, features],
                            rhs=codes[:, tokens].bitcast(FP8X4),
                            rhs_scale=scales[:, tokens],
                            start=side == 0,
                            stop=side == 1,
                        )
            for c in range(CHUNKS):
                nc.scalar.activation(
                    out=gate[g][:, c, tokens],
                    in_=gate_banks[c][:, tokens],
                    func=ACT.Sigmoid,
                    bias=b_gate_bf[:, c : c + 1],
                    scale=1.0,
                )

        def multiply(g, tokens, chunks, engine):
            for c in chunks:
                engine.tensor_tensor(
                    out=update[g][:, c, tokens],
                    in0=gate[g][:, c, tokens],
                    in1=difference[g][:, c, tokens],
                    op=ALU.mult,
                )

        def transpose_back(g, a):
            bank = banks.tile([P, CHUNKS, P], F32, name="back_bank", tag="bank")
            n = g * GROUP_TILES + a

            def transpose(c):
                nc.tensor.transpose(bank[:, c, :], update[g][:, c, a * P : (a + 1) * P], identity[:])
                if c == CHUNKS - 1:
                    result = ring.tile([P, FEATURES], F32, bufs=4)
                    nc.vector.tensor_tensor(
                        out=result[:].rearrange("r (u p e) -> r u p e", u=2, e=2),
                        in0=bank[:].rearrange("r (u e) p -> r u p e", u=2),
                        in1=x_rows[:, n, :].rearrange("r (u p e) -> r u p e", u=2, e=2),
                        op=ALU.add,
                    )
                    nc.sync.dma_start(out=out_dram[:, n, :], in_=result[:])

            return transpose

        first_half, second_half = slice(0, GROUP // 2), slice(GROUP // 2, GROUP)

        def step(s):
            start_routed(s)
            more_x = s + 2 < GROUPS
            if s == 1:
                start_x(2)
            if more_x:
                start_x(s + 2)
            for a in range(GROUP_TILES):
                jobs = []
                if s >= 2 and a == 3:
                    jobs.append(transpose_back(s - 2, a))
                routed_bank = new_routed_bank()
                if s >= 2 and a < 3:
                    jobs.append(transpose_back(s - 2, a))
                if s == 1 and a == 0:
                    jobs += [transpose_x(2, 0), transpose_x(2, 1)]
                if more_x and a in (1, 2):
                    jobs.append(transpose_x(s + 2, a - 1))
                if a == 3:
                    quantise_routed(s, slice(0, 2 * P))
                    quantise_routed(s, slice(2 * P, 3 * P))
                    if more_x:
                        quantise_x(s + 2, bank_columns(0))
                first_gap = 1 if a == 0 else 0
                last_gap = CHUNKS - 2 if a == 3 else CHUNKS - 1
                mix_limbs(s, a, routed_bank, jobs, range(first_gap, last_gap + 1))
                if s == 1 and a == 2:
                    quantise_x(2, slice(0, GROUP))
                if a == 3:
                    quantise_routed(s, slice(3 * P, GROUP))
                    if more_x:
                        quantise_x(s + 2, bank_columns(1))
                subtract_x(s, a, routed_bank)
            project_all(s + 1)
            start_gate(s)
            open_gate(s, slice(0, GROUP))
            multiply(s, slice(0, GROUP), range(CHUNKS), nc.gpsimd)

        def project_all(g):
            start_projected(g)
            projected_banks = [project(g, a) for a in range(GROUP_TILES)]
            for a in range(GROUP_TILES):
                add_route_bias(g, a, projected_banks[a])

        gate_grouped = keep.tile([P, 2, FEATURES, PACK], BF16, align_bytes=64)
        gate_codes = keep.tile([P, 2, FEATURES], U32, align_bytes=64)
        gate_scales = keep.tile([P, 2, FEATURES], U8, align_bytes=64)
        gate_words = gate_rows[:].bitcast(F32)

        def transpose_gate(side, half):
            words = gate_words[:, 2 * half : 2 * half + 2, side * 2 * P : (side + 1) * 2 * P]
            return transpose_rows(words, gate_grouped[:, side, bank_columns(half), :])

        def quantise_gate(side, half):
            columns = bank_columns(half)
            quantise(gate_grouped[:, side, columns, :], gate_codes[:, side, columns], gate_scales[:, side, columns])

        sums_bank = banks.tile([P, FEATURES], F32, tag="bank")
        nc.tensor.matmul(
            out=sums_bank[:, 0:LIMBS],
            lhsT=same_block[:].rearrange("q b j -> q (b j)"),
            rhs=tanh[:],
            start=True,
            stop=True,
        )
        start_projected(0)
        first_banks = [project(0, a) for a in range(GROUP_TILES)]
        run(transpose_x(1, 0))
        run(transpose_x(1, 1))
        row_sum = keep.tile([P, LIMBS], F32)
        inverse = keep.tile([P, LIMBS], F32)
        weights = keep.tile([P, LIMBS], F32)
        nc.vector.tensor_scalar_add(out=row_sum[:], in0=sums_bank[:, 0:LIMBS], scalar1=LIMBS + 2e-6)
        nc.vector.reciprocal(out=inverse[:], in_=row_sum[:])
        nc.vector.scalar_tensor_tensor(
            out=weights[:], in0=tanh[:], scalar=1.0, in1=inverse[:], op0=ALU.add, op1=ALU.mult
        )
        add_route_bias(0, 0, first_banks[0])
        nc.vector.tensor_tensor(
            out=mixer[:],
            in0=same_position[:].unsqueeze(2).to_broadcast(block_shape),
            in1=weights[:].unsqueeze(1).to_broadcast(block_shape),
            op=ALU.mult,
        )
        add_route_bias(0, 1, first_banks[1])
        add_route_bias(0, 2, first_banks[2])
        add_route_bias(0, 3, first_banks[3])
        quantise_x(1, slice(0, GROUP))
        start_routed(0)
        for a in range(GROUP_TILES):
            routed_bank = new_routed_bank()
            jobs = [transpose_gate(0, a), transpose_gate(1, a)] if a < 2 else []
            mix_limbs(0, a, routed_bank, jobs)
            if a == 3:
                quantise_routed(0, slice(0, GROUP))
            if a < 2:
                quantise_gate(0, a)
            subtract_x(0, a, routed_bank)
            if a < 2:
                quantise_gate(1, a)
        project_all(1)
        start_gate(0)
        open_gate(0, slice(0, GROUP))
        multiply(0, slice(0, GROUP), (0, 1), nc.gpsimd)
        multiply(0, slice(0, GROUP), (2, 3), nc.vector)

        for s in range(1, GROUPS - 1):
            step(s)

        last = GROUPS - 1
        start_routed(last)
        ways_back = [[(last - 2, 0), (last - 2, 1)], [(last - 2, 2), (last - 2, 3)], [], [(last - 1, 0), (last - 1, 1)]]
        for a in range(GROUP_TILES):
            routed_bank = new_routed_bank()
            jobs = [transpose_back(*back) for back in ways_back[a]]
            mix_limbs(last, a, routed_bank, jobs, [2, 3] if a == 3 else range(CHUNKS))
            if a == 2:
                quantise_routed(last, first_half)
            if a == 3:
                quantise_routed(last, second_half)
            subtract_x(last, a, routed_bank)
        start_gate(last)
        open_gate(last, first_half)
        multiply(last, first_half, (0, 1), nc.gpsimd)
        run(transpose_back(last - 1, 2))
        run(transpose_back(last - 1, 3))
        multiply(last, first_half, (2, 3), nc.vector)
        open_gate(last, second_half)
        multiply(last, second_half, range(CHUNKS), nc.vector)
        for a in range(GROUP_TILES):
            run(transpose_back(last, a))
